import numpy as np
import ml_dtypes


def mxq(x, axis, fmt="e4m3"):
    dtype, down = {"e4m3": (ml_dtypes.float8_e4m3fn, 7), "e5m2": (ml_dtypes.float8_e5m2, 14)}[fmt]
    v = np.moveaxis(np.asarray(x, np.float32).astype(ml_dtypes.bfloat16).astype(np.float64), axis, -1)
    blocks = v.reshape(v.shape[:-1] + (-1, 32))
    amax = np.abs(blocks).max(-1, keepdims=True)
    byte = np.maximum(np.where(amax > 0, np.frexp(amax)[1] - 1 + 127, 0) - down, 1)
    scale = np.exp2(byte - 127.0)
    codes = (blocks / scale).astype(np.float32).astype(dtype).astype(np.float64)
    return np.moveaxis((codes * scale).reshape(v.shape), -1, axis)


WIDE = False


def mx_kscale(k):
    if not WIDE:
        return np.ones(k)
    levels = np.array([10, -10, 5, -5, 0])
    if k % 512:
        return np.exp2(np.random.permutation(np.resize(levels, k // 32))).repeat(32)
    a = np.empty((k // 512, 16))
    for p in range(k // 512):
        a[p, :8] = np.random.permutation(np.resize(levels, 8))
        for g in range(8):
            far = levels[np.abs(levels - a[p, g]) >= 10]
            a[p, g + 8] = far[np.random.randint(len(far))]
    return np.exp2(a.ravel()).repeat(32)


BF16 = ml_dtypes.bfloat16


def bf(x):
    return np.asarray(x, np.float32).astype(BF16)


def f64(x):
    return np.asarray(x).astype(np.float64)


B, T, D, H, KH, F = 2, 128, 1024, 8, 2, 4096
EPS = 1e-5


def layer_norm(v, g, b):
    m = v.mean(-1, keepdims=True)
    var = ((v - m) ** 2).mean(-1, keepdims=True)
    return (v - m) / np.sqrt(var + EPS) * g + b


def setup_inputs():
    s, t = mx_kscale(D), mx_kscale(D)
    return {
        "h_attn": bf(np.random.standard_normal((B, T, D)) * 0.4 * s),
        "x": bf(np.random.standard_normal((B, T, D))),
        "Wo": bf(np.random.standard_normal((D, D)) * 2.0 / np.sqrt(D) / s[:, None]),
        "bo": bf(np.random.standard_normal(D) * 0.2),
        "ln2_g": bf(1.5 + 0.3 * np.random.standard_normal(D)),
        "ln2_b": bf(0.3 + 0.3 * np.random.standard_normal(D)),
        "fln_g": bf((1.0 + 0.1 * np.random.standard_normal(D)) * t),
        "fln_b": bf(0.2 * np.random.standard_normal(D) * t),
        "W1": bf(np.random.standard_normal((D, F)) / np.sqrt(D) / t[:, None]),
        "b1": bf(np.random.standard_normal(F) * 0.3),
        "W2": bf(np.random.standard_normal((D, F)) / np.sqrt(D) / t[:, None]),
        "b2": bf(np.random.standard_normal(F) * 0.3),
    }


def reference(h_attn, x, Wo, bo, ln2_g, ln2_b, fln_g, fln_b, W1, b1, W2, b2):
    y = f64(x) + ((mxq(f64(h_attn), 2, "e4m3") @ mxq(f64(Wo), 0, "e4m3")) + f64(bo))
    r = layer_norm(y, f64(ln2_g), f64(ln2_b))
    h2q = mxq(layer_norm(r, f64(fln_g), f64(fln_b)), 2, "e4m3")
    g_pre = (h2q @ mxq(f64(W1), 0, "e4m3")) + f64(b1)
    hidden = (h2q @ mxq(f64(W2), 0, "e4m3")) + f64(b2)
    return r, g_pre, hidden

@@ -1,0 +1,337 @@
+from contextlib import ExitStack
+
+import concourse.mybir as mybir
+from concourse.masks import make_identity
+
+F32 = mybir.dt.float32
+BF16 = mybir.dt.bfloat16
+U32 = mybir.dt.uint32
+U8 = mybir.dt.uint8
+FP8X4 = mybir.dt.float8_e4m3fn_x4
+ALU = mybir.AluOpType
+ACT = mybir.ActivationFunctionType
+
+P = 128
+PACK = 4
+K_PASS = P * PACK
+TOKENS = 256
+TOKEN_TILES = TOKENS // P
+D = 1024
+F = 4096
+PASSES = D // K_PASS
+K_BLOCKS = D // P
+BANK = 512
+PSUM_BANKS = 8
+UNIT_COLS = 1024
+UNIT_BANKS = UNIT_COLS // BANK
+RAW_BUFS = 8
+RUN = 4
+TOGETHER_COLS = 672
+STEADY_COLS = 256
+LAG = 2
+EPS = 1e-5
+
+FLOPS = 2 * TOKENS * D * (D + 2 * F)
+
+
+def tile_transformerblock_pa_kernel(
+    tc, h_attn, x, Wo, bo, ln2_g, ln2_b, fln_g, fln_b, W1, b1, W2, b2, out_0, out_1, out_2
+):
+    nc = tc.nc
+    r_out = out_0.flatten_outer_dims()
+
+    units = []
+    for w, width in ((Wo, D), (W1, F), (W2, F)):
+        for first_col in range(0, width, UNIT_COLS):
+            for g in range(PASSES):
+                units.append((w, first_col, g))
+    last_chunk = len(units) // PASSES - 1
+
+    with ExitStack() as ctx:
+        consts = ctx.enter_context(tc.tile_pool(name="consts", bufs=1))
+        small = ctx.enter_context(tc.tile_pool(name="small", bufs=2))
+        rows = ctx.enter_context(tc.tile_pool(name="rows", bufs=4))
+        acts = ctx.enter_context(tc.tile_pool(name="acts", bufs=2))
+        raw_pool = ctx.enter_context(tc.tile_pool(name="raw", bufs=RAW_BUFS))
+        grouped_pool = ctx.enter_context(tc.tile_pool(name="grouped", bufs=4))
+        quantised = ctx.enter_context(tc.tile_pool(name="quantised", bufs=6))
+        staged_pool = ctx.enter_context(tc.tile_pool(name="staged", bufs=4))
+        psum = ctx.enter_context(tc.psum_pool(name="psum", bufs=PSUM_BANKS))
+        ctx.enter_context(tc.manual_schedule())
+
+        raw = {}
+        grouped = {}
+        packed = {}
+        banks = {}
+
+        def load_as_rows(key, vectors):
+            vec_rows = consts.tile([P, BANK], BF16, name="rows_" + key)
+            nc.vector.memset(vec_rows[:], 0.0)
+            first_row = []
+            next_row = 0
+            for vec in vectors:
+                n_rows = vec.shape[0] // BANK
+                nc.sync.dma_start(
+                    out=vec_rows[next_row : next_row + n_rows, :],
+                    in_=vec.rearrange("(r c) -> r c", c=BANK),
+                )
+                first_row.append(next_row)
+                next_row += n_rows
+            return vec_rows, first_row
+
+        def spread(key, vec_rows, first_row, width, copy_out):
+            everywhere = consts.tile([P, width], BF16, name="everywhere_" + key)
+            for pair in range(width // (2 * BANK)):
+                bank = psum.tile([P, 2 * BANK], BF16, tag="bank")
+                for s in range(2):
+                    r = first_row + 2 * pair + s
+                    nc.tensor.matmul(
+                        out=bank[:, s * BANK : (s + 1) * BANK],
+                        lhsT=ident[:, r : r + 1].to_broadcast([P, P]),
+                        rhs=vec_rows[:],
+                        start=True,
+                        stop=True,
+                    )
+                copy_out(out=everywhere[:, pair * 2 * BANK : (pair + 1) * 2 * BANK], in_=bank[:])
+            return everywhere
+
+        def flip_tokens(token_rows):
+            flipped = psum.tile([P, K_BLOCKS, P], BF16, tag="bank")
+            for kb in range(K_BLOCKS):
+                g, t = divmod(kb, PACK)
+                nc.tensor.transpose(
+                    flipped[:, kb, :], token_rows[:, g * K_PASS + t : (g + 1) * K_PASS : PACK], ident[:]
+                )
+            token_grouped = acts.tile([P, PASSES, P, PACK], BF16, tag="token_grouped", align_bytes=64)
+            nc.scalar.copy(
+                out=token_grouped[:], in_=flipped[:].rearrange("p (g t) r -> p g r t", t=PACK)
+            )
+            return token_grouped
+
+        def quantise_tokens(key, token_grouped):
+            codes = consts.tile([P, PASSES * P], U32, name="codes_" + key, align_bytes=64)
+            scales = consts.tile([P, PASSES * P], U8, name="scales_" + key, align_bytes=64)
+            nc.vector.quantize_mx(
+                out=codes[:].bitcast(FP8X4),
+                scales=scales[:],
+                in_=token_grouped[:].rearrange("p g r t -> p (g r t)"),
+            )
+            return codes, scales
+
+        def load(u):
+            w, first_col, g = units[u]
+            rows_of_unit = raw_pool.tile([P, PACK, UNIT_COLS], BF16, tag="raw")
+            nc.sync.dma_start(
+                out=rows_of_unit[:],
+                in_=w[g * K_PASS : (g + 1) * K_PASS, first_col : first_col + UNIT_COLS].rearrange(
+                    "(p t) n -> p t n", p=P
+                ),
+            )
+            raw[u] = rows_of_unit
+
+        def regroup(u, vector_cols):
+            side_by_side = grouped_pool.tile([P, UNIT_COLS, PACK], BF16, tag="grouped", align_bytes=64)
+            dst = side_by_side[:].rearrange("p (c i) t -> p c t i", i=RUN)
+            src = raw[u][:].rearrange("p t (c i) -> p c t i", i=RUN)
+            split = vector_cols // RUN
+            if split > 0:
+                nc.vector.tensor_copy(out=dst[:, :split], in_=src[:, :split])
+            if split < UNIT_COLS // RUN:
+                nc.scalar.copy(out=dst[:, split:], in_=src[:, split:])
+            grouped[u] = side_by_side
+            if u + RAW_BUFS < len(units):
+                load(u + RAW_BUFS)
+
+        def quantise(u):
+            codes = quantised.tile([P, UNIT_COLS], U32, tag="codes", align_bytes=64)
+            scales = quantised.tile([P, UNIT_COLS], U8, tag="scales", align_bytes=64)
+            nc.vector.quantize_mx(
+                out=codes[:].bitcast(FP8X4),
+                scales=scales[:],
+                in_=grouped[u][:].rearrange("p n t -> p (n t)"),
+            )
+            packed[u] = (codes, scales)
+
+        def multiply(u, tokens_q):
+            chunk, g = divmod(u, PASSES)
+            w_codes, w_scales = packed[u]
+            for m in range(TOKEN_TILES):
+                token_codes, token_scales = tokens_q[m]
+                for n in range(UNIT_BANKS):
+                    if g == 0:
+                        acc = psum.tile([P, BANK], F32, tag="bank")
+                        banks[(chunk, m, n)] = acc
+                    nc.tensor.matmul_mx(
+                        out=banks[(chunk, m, n)][:],
+                        lhsT=token_codes[:, g * P : (g + 1) * P].bitcast(FP8X4),
+                        lhsT_scale=token_scales[:, g * P : (g + 1) * P],
+                        rhs=w_codes[:, n * BANK : (n + 1) * BANK].bitcast(FP8X4),
+                        rhs_scale=w_scales[:, n * BANK : (n + 1) * BANK],
+                        start=(g == 0),
+                        stop=(g == PASSES - 1),
+                    )
+
+        def new_statistics():
+            half_sums = small.tile([P, TOKEN_TILES, UNIT_BANKS], F32, tag="half_sums")
+            minus_mean = small.tile([P, TOKEN_TILES, 1], F32, tag="minus_mean")
+            sum_sq = small.tile([P, TOKEN_TILES, 1], F32, tag="sum_sq")
+            return half_sums, minus_mean, sum_sq
+
+        def measure(m, src, half_sums, minus_mean, sum_sq):
+            nc.vector.tensor_scalar(
+                out=minus_mean[:, m, :],
+                in0=half_sums[:, m, 0:1],
+                scalar1=half_sums[:, m, 1:2],
+                scalar2=-1.0 / D,
+                op0=ALU.add,
+                op1=ALU.mult,
+            )
+            squares = acts.tile([P, D], BF16, tag="squares")
+            nc.scalar.activation(
+                out=squares[:],
+                in_=src[:],
+                func=ACT.Square,
+                bias=minus_mean[:, m, :],
+                accum_out=sum_sq[:, m, :],
+            )
+
+        def rstd_of(sum_sq):
+            var_eps = small.tile([P, TOKEN_TILES, 1], F32, tag="var_eps")
+            nc.gpsimd.tensor_scalar(
+                out=var_eps[:], in0=sum_sq[:], scalar1=1.0 / D, scalar2=EPS, op0=ALU.mult, op1=ALU.add
+            )
+            rstd = small.tile([P, TOKEN_TILES, 1], F32, tag="rstd")
+            nc.gpsimd.tensor_tensor(out=rstd[:], in0=var_eps[:], in1=minus_half[:], op=ALU.pow)
+            return rstd
+
+        def centre_times_gain(dest, src, minus_mean, gain):
+            nc.vector.scalar_tensor_tensor(
+                out=dest[:], in0=src[:], scalar=minus_mean, in1=gain[:], op0=ALU.add, op1=ALU.mult
+            )
+
+        ident = consts.tile([P, P], BF16)
+        make_identity(nc, ident[:])
+        minus_half = consts.tile([P, TOKEN_TILES, 1], F32)
+        nc.vector.memset(minus_half[:], -0.5)
+
+        norm_rows, norm_first = load_as_rows("norm", (bo, ln2_g, ln2_b, fln_g, fln_b))
+        h_sb = consts.tile([P, TOKEN_TILES, D], BF16)
+        nc.sync.dma_start(
+            out=h_sb[:], in_=h_attn.flatten_outer_dims().rearrange("(m p) d -> p m d", p=P)
+        )
+        x_sb = consts.tile([P, TOKEN_TILES, D], BF16)
+        nc.sync.dma_start(out=x_sb[:], in_=x.flatten_outer_dims().rearrange("(m p) d -> p m d", p=P))
+        for u in range(PASSES):
+            load(u)
+        bias_rows, bias_first = load_as_rows("bias", (b1, b2))
+        for u in range(PASSES, RAW_BUFS):
+            load(u)
+
+        bo_all = spread("bo", norm_rows, norm_first[0], D, nc.vector.tensor_copy)
+        x_plus_bo = []
+        for m in range(TOKEN_TILES):
+            sum_row = rows.tile([P, D], F32, tag="row")
+            nc.vector.tensor_tensor(out=sum_row[:], in0=x_sb[:, m, :], in1=bo_all[:], op=ALU.add)
+            x_plus_bo.append(sum_row)
+        h_grouped = [flip_tokens(h_sb[:, m, :]) for m in range(TOKEN_TILES)]
+        h_q = [quantise_tokens("h%d" % m, h_grouped[m]) for m in range(TOKEN_TILES)]
+        ln2_g_all = spread("ln2_g", norm_rows, norm_first[1], D, nc.scalar.copy)
+        regroup(0, TOGETHER_COLS)
+        ln2_b_all = spread("ln2_b", norm_rows, norm_first[2], D, nc.scalar.copy)
+        quantise(0)
+        multiply(0, h_q)
+        regroup(1, TOGETHER_COLS)
+        quantise(1)
+        multiply(1, h_q)
+
+        regroup(2, 0)
+        half_sums, minus_mean, sum_sq = new_statistics()
+        r = []
+        for m in range(TOKEN_TILES):
+            r_row = rows.tile([P, D], F32, tag="row")
+            for n in range(UNIT_BANKS):
+                cols = slice(n * BANK, (n + 1) * BANK)
+                nc.vector.scalar_tensor_tensor(
+                    out=r_row[:, cols],
+                    in0=banks[(0, m, n)][:],
+                    scalar=1.0,
+                    in1=x_plus_bo[m][:, cols],
+                    op0=ALU.mult,
+                    op1=ALU.add,
+                    accum_out=half_sums[:, m, n : n + 1],
+                )
+            measure(m, r_row, half_sums, minus_mean, sum_sq)
+            r.append(r_row)
+        rstd = rstd_of(sum_sq)
+        fln_g_all = spread("fln_g", norm_rows, norm_first[3], D, nc.scalar.copy)
+        fln_b_all = spread("fln_b", norm_rows, norm_first[4], D, nc.scalar.copy)
+        for m in range(TOKEN_TILES):
+            centre_times_gain(r[m], r[m], minus_mean[:, m, :], ln2_g_all)
+        quantise(2)
+        b1_all = spread("b1", bias_rows, bias_first[0], F, nc.scalar.copy)
+        half_sums, minus_mean, sum_sq = new_statistics()
+        for m in range(TOKEN_TILES):
+            for n in range(UNIT_BANKS):
+                cols = slice(n * BANK, (n + 1) * BANK)
+                nc.vector.scalar_tensor_tensor(
+                    out=r[m][:, cols],
+                    in0=r[m][:, cols],
+                    scalar=rstd[:, m, :],
+                    in1=ln2_b_all[:, cols],
+                    op0=ALU.mult,
+                    op1=ALU.add,
+                    accum_out=half_sums[:, m, n : n + 1],
+                )
+            nc.sync.dma_start(out=r_out[m * P : (m + 1) * P, :], in_=r[m][:])
+            measure(m, r[m], half_sums, minus_mean, sum_sq)
+        rstd = rstd_of(sum_sq)
+        centred = []
+        for m in range(TOKEN_TILES):
+            centred_row = rows.tile([P, D], F32, tag="row")
+            centre_times_gain(centred_row, r[m], minus_mean[:, m, :], fln_g_all)
+            centred.append(centred_row)
+        regroup(3, 0)
+        h2_grouped = []
+        for m in range(TOKEN_TILES):
+            h2 = acts.tile([P, D], BF16, tag="h2")
+            nc.vector.scalar_tensor_tensor(
+                out=h2[:],
+                in0=centred[m][:],
+                scalar=rstd[:, m, :],
+                in1=fln_b_all[:],
+                op0=ALU.mult,
+                op1=ALU.add,
+            )
+            h2_grouped.append(flip_tokens(h2))
+        b2_all = spread("b2", bias_rows, bias_first[1], F, nc.scalar.copy)
+        regroup(4, UNIT_COLS)
+        regroup(5, UNIT_COLS)
+        quantise(3)
+        h2_q = [quantise_tokens("h2_%d" % m, h2_grouped[m]) for m in range(TOKEN_TILES)]
+
+        def finish(chunk, m):
+            w, first_col, g = units[chunk * PASSES]
+            out, bias = (out_1, b1_all) if w is W1 else (out_2, b2_all)
+            staged = staged_pool.tile([P, UNIT_COLS], F32, tag="staged")
+            for n in range(UNIT_BANKS):
+                nc.vector.tensor_tensor(
+                    out=staged[:, n * BANK : (n + 1) * BANK],
+                    in0=banks[(chunk, m, n)][:],
+                    in1=bias[:, first_col + n * BANK : first_col + (n + 1) * BANK],
+                    op=ALU.add,
+                )
+            nc.sync.dma_start(
+                out=out.flatten_outer_dims()[m * P : (m + 1) * P, first_col : first_col + UNIT_COLS],
+                in_=staged[:],
+            )
+
+        for u in range(PASSES, 2 * PASSES):
+            multiply(u, h2_q)
+        for u in range(3 * PASSES, len(units) + LAG):
+            quantise(u - LAG)
+            multiply(u - LAG, h2_q)
+            if u < len(units):
+                regroup(u, STEADY_COLS)
+            finish((u - LAG - PASSES) // PASSES, u % TOKEN_TILES)
+        for m in range(TOKEN_TILES):
+            finish(last_chunk, m)

@@ -19,17 +19,13 @@ TOKEN_TILES = TOKENS // P
 D = 1024
 F = 4096
 PASSES = D // K_PASS
-K_BLOCKS = D // P
 BANK = 512
-PSUM_BANKS = 8
-UNIT_COLS = 1024
-UNIT_BANKS = UNIT_COLS // BANK
+CHUNK = 1024
 RAW_BUFS = 8
 RUN = 4
-TOGETHER_COLS = 672
-STEADY_COLS = 256
-LAG = 2
 EPS = 1e-5
+VECTOR_COLS = [0, 0, 416, 416, 416, 416, 416, 416, 416]
+POOL_COLS = [0, 512, 0, 400, 400, 400, 400, 400, 400]
 
 FLOPS = 2 * TOKENS * D * (D + 2 * F)
 
@@ -40,12 +36,12 @@ def tile_transformerblock_pa_kernel(
     nc = tc.nc
     r_out = out_0.flatten_outer_dims()
 
-    units = []
-    for w, width in ((Wo, D), (W1, F), (W2, F)):
-        for first_col in range(0, width, UNIT_COLS):
-            for g in range(PASSES):
-                units.append((w, first_col, g))
-    last_chunk = len(units) // PASSES - 1
+    chunks = [(Wo, 0)]
+    for w in (W1, W2):
+        for first_col in range(0, F, CHUNK):
+            chunks.append((w, first_col))
+    last = len(chunks) - 1
+    pieces = {"A": (0, 0, CHUNK), "B": (1, 0, BANK), "C": (1, BANK, BANK)}
 
     with ExitStack() as ctx:
         consts = ctx.enter_context(tc.tile_pool(name="consts", bufs=1))
@@ -53,58 +49,63 @@ def tile_transformerblock_pa_kernel(
         rows = ctx.enter_context(tc.tile_pool(name="rows", bufs=4))
         acts = ctx.enter_context(tc.tile_pool(name="acts", bufs=2))
         raw_pool = ctx.enter_context(tc.tile_pool(name="raw", bufs=RAW_BUFS))
-        grouped_pool = ctx.enter_context(tc.tile_pool(name="grouped", bufs=4))
-        quantised = ctx.enter_context(tc.tile_pool(name="quantised", bufs=6))
+        grouped_pool = ctx.enter_context(tc.tile_pool(name="grouped", bufs=2))
+        quantised = ctx.enter_context(tc.tile_pool(name="quantised", bufs=4))
         staged_pool = ctx.enter_context(tc.tile_pool(name="staged", bufs=4))
-        psum = ctx.enter_context(tc.psum_pool(name="psum", bufs=PSUM_BANKS))
+        psum = ctx.enter_context(tc.psum_pool(name="psum", bufs=4))
         ctx.enter_context(tc.manual_schedule())
 
         raw = {}
         grouped = {}
         packed = {}
         banks = {}
+        loaded = []
 
-        def load_as_rows(key, vectors):
-            vec_rows = consts.tile([P, BANK], BF16, name="rows_" + key)
-            nc.vector.memset(vec_rows[:], 0.0)
-            first_row = []
-            next_row = 0
-            for vec in vectors:
-                n_rows = vec.shape[0] // BANK
-                nc.sync.dma_start(
-                    out=vec_rows[next_row : next_row + n_rows, :],
-                    in_=vec.rearrange("(r c) -> r c", c=BANK),
+        def load_next():
+            c, g = divmod(len(loaded), PASSES)
+            if c > last:
+                return
+            w, first_col = chunks[c]
+            rows_of_pass = raw_pool.tile([P, PACK, CHUNK], BF16, tag="raw")
+            nc.sync.dma_start(
+                out=rows_of_pass[:],
+                in_=w[g * K_PASS : (g + 1) * K_PASS, first_col : first_col + CHUNK].rearrange(
+                    "(p t) n -> p t n", p=P
+                ),
+            )
+            raw[(c, g)] = rows_of_pass
+            loaded.append((c, g))
+
+        def spread(first, tag):
+            bank = psum.tile([P, 2 * BANK], BF16, tag=tag)
+            for s in range(2):
+                row = first + s
+                nc.tensor.matmul(
+                    out=bank[:, s * BANK : (s + 1) * BANK],
+                    lhsT=ident[:, row : row + 1].to_broadcast([P, P]),
+                    rhs=vec_rows[:],
+                    start=True,
+                    stop=True,
                 )
-                first_row.append(next_row)
-                next_row += n_rows
-            return vec_rows, first_row
-
-        def spread(key, vec_rows, first_row, width, copy_out):
-            everywhere = consts.tile([P, width], BF16, name="everywhere_" + key)
-            for pair in range(width // (2 * BANK)):
-                bank = psum.tile([P, 2 * BANK], BF16, tag="bank")
-                for s in range(2):
-                    r = first_row + 2 * pair + s
-                    nc.tensor.matmul(
-                        out=bank[:, s * BANK : (s + 1) * BANK],
-                        lhsT=ident[:, r : r + 1].to_broadcast([P, P]),
-                        rhs=vec_rows[:],
-                        start=True,
-                        stop=True,
-                    )
-                copy_out(out=everywhere[:, pair * 2 * BANK : (pair + 1) * 2 * BANK], in_=bank[:])
-            return everywhere
+            return bank
 
         def flip_tokens(token_rows):
-            flipped = psum.tile([P, K_BLOCKS, P], BF16, tag="bank")
-            for kb in range(K_BLOCKS):
-                g, t = divmod(kb, PACK)
-                nc.tensor.transpose(
-                    flipped[:, kb, :], token_rows[:, g * K_PASS + t : (g + 1) * K_PASS : PACK], ident[:]
-                )
+            words = token_rows.bitcast(F32)
+            flipped = psum.tile([P, PASSES * 2, P], F32, tag="even")
+            for g in range(PASSES):
+                for u in range(2):
+                    nc.tensor.transpose(
+                        flipped[:, 2 * g + u, :],
+                        words[:, g * 2 * P + u : (g + 1) * 2 * P : 2],
+                        ident_words[:],
+                    )
+            return flipped
+
+        def group_tokens(flipped):
             token_grouped = acts.tile([P, PASSES, P, PACK], BF16, tag="token_grouped", align_bytes=64)
             nc.scalar.copy(
-                out=token_grouped[:], in_=flipped[:].rearrange("p (g t) r -> p g r t", t=PACK)
+                out=token_grouped[:].bitcast(F32),
+                in_=flipped[:].rearrange("p (g u) r -> p g r u", u=2),
             )
             return token_grouped
 
@@ -118,74 +119,70 @@ def tile_transformerblock_pa_kernel(
             )
             return codes, scales
 
-        def load(u):
-            w, first_col, g = units[u]
-            rows_of_unit = raw_pool.tile([P, PACK, UNIT_COLS], BF16, tag="raw")
-            nc.sync.dma_start(
-                out=rows_of_unit[:],
-                in_=w[g * K_PASS : (g + 1) * K_PASS, first_col : first_col + UNIT_COLS].rearrange(
-                    "(p t) n -> p t n", p=P
-                ),
-            )
-            raw[u] = rows_of_unit
+        def regroup(engine, c, piece, lo, hi):
+            if lo >= hi:
+                return
+            g, first, width = pieces[piece]
+            if (c, piece) not in grouped:
+                if piece == "C":
+                    slot = "C%d" % (1 if c == 0 else c % 2)
+                    side_by_side = grouped_pool.tile([P, width, PACK], BF16, tag=slot, bufs=1, align_bytes=64)
+                else:
+                    side_by_side = grouped_pool.tile([P, width, PACK], BF16, tag=piece, align_bytes=64)
+                grouped[(c, piece)] = side_by_side
+            dst = grouped[(c, piece)][:, lo:hi, :]
+            src = raw[(c, g)][:, :, first + lo : first + hi]
+            if engine == "pool":
+                nc.gpsimd.tensor_scalar(
+                    out=dst,
+                    in0=src.rearrange("p t n -> p n t"),
+                    scalar1=1.0,
+                    scalar2=0.0,
+                    op0=ALU.mult,
+                    op1=ALU.add,
+                )
+                return
+            dst = dst.rearrange("p (c i) t -> p c t i", i=RUN)
+            src = src.rearrange("p t (c i) -> p c t i", i=RUN)
+            if engine == "vector":
+                nc.vector.tensor_copy(out=dst, in_=src)
+            else:
+                nc.scalar.copy(out=dst, in_=src)
 
-        def regroup(u, vector_cols):
-            side_by_side = grouped_pool.tile([P, UNIT_COLS, PACK], BF16, tag="grouped", align_bytes=64)
-            dst = side_by_side[:].rearrange("p (c i) t -> p c t i", i=RUN)
-            src = raw[u][:].rearrange("p t (c i) -> p c t i", i=RUN)
-            split = vector_cols // RUN
-            if split > 0:
-                nc.vector.tensor_copy(out=dst[:, :split], in_=src[:, :split])
-            if split < UNIT_COLS // RUN:
-                nc.scalar.copy(out=dst[:, split:], in_=src[:, split:])
-            grouped[u] = side_by_side
-            if u + RAW_BUFS < len(units):
-                load(u + RAW_BUFS)
-
-        def quantise(u):
-            codes = quantised.tile([P, UNIT_COLS], U32, tag="codes", align_bytes=64)
-            scales = quantised.tile([P, UNIT_COLS], U8, tag="scales", align_bytes=64)
+        def quantise(c, piece):
+            g, first, width = pieces[piece]
+            if c not in packed:
+                codes = quantised.tile([P, PASSES, CHUNK], U32, tag="codes", align_bytes=64)
+                scales = quantised.tile([P, PASSES, CHUNK], U8, tag="scales", align_bytes=64)
+                packed[c] = (codes, scales)
+            codes, scales = packed[c]
             nc.vector.quantize_mx(
-                out=codes[:].bitcast(FP8X4),
-                scales=scales[:],
-                in_=grouped[u][:].rearrange("p n t -> p (n t)"),
+                out=codes[:, g, first : first + width].bitcast(FP8X4),
+                scales=scales[:, g, first : first + width],
+                in_=grouped[(c, piece)][:].rearrange("p n t -> p (n t)"),
             )
-            packed[u] = (codes, scales)
 
-        def multiply(u, tokens_q):
-            chunk, g = divmod(u, PASSES)
-            w_codes, w_scales = packed[u]
-            for m in range(TOKEN_TILES):
-                token_codes, token_scales = tokens_q[m]
-                for n in range(UNIT_BANKS):
-                    if g == 0:
-                        acc = psum.tile([P, BANK], F32, tag="bank")
-                        banks[(chunk, m, n)] = acc
+        def multiply(c, piece, tokens_q):
+            g, first, width = pieces[piece]
+            codes, scales = packed[c]
+            for n in range(first // BANK, (first + width) // BANK):
+                for m in range(TOKEN_TILES):
+                    opened = (c, m, n) in banks
+                    if not opened:
+                        acc = psum.tile([P, BANK], F32, tag=("odd" if c % 2 == 0 and c > 0 else "even"))
+                        banks[(c, m, n)] = acc
+                    token_codes, token_scales = tokens_q[m]
                     nc.tensor.matmul_mx(
-                        out=banks[(chunk, m, n)][:],
+                        out=banks[(c, m, n)][:],
                         lhsT=token_codes[:, g * P : (g + 1) * P].bitcast(FP8X4),
                         lhsT_scale=token_scales[:, g * P : (g + 1) * P],
-                        rhs=w_codes[:, n * BANK : (n + 1) * BANK].bitcast(FP8X4),
-                        rhs_scale=w_scales[:, n * BANK : (n + 1) * BANK],
-                        start=(g == 0),
-                        stop=(g == PASSES - 1),
+                        rhs=codes[:, g, n * BANK : (n + 1) * BANK].bitcast(FP8X4),
+                        rhs_scale=scales[:, g, n * BANK : (n + 1) * BANK],
+                        start=not opened,
+                        stop=opened,
                     )
 
-        def new_statistics():
-            half_sums = small.tile([P, TOKEN_TILES, UNIT_BANKS], F32, tag="half_sums")
-            minus_mean = small.tile([P, TOKEN_TILES, 1], F32, tag="minus_mean")
-            sum_sq = small.tile([P, TOKEN_TILES, 1], F32, tag="sum_sq")
-            return half_sums, minus_mean, sum_sq
-
-        def measure(m, src, half_sums, minus_mean, sum_sq):
-            nc.vector.tensor_scalar(
-                out=minus_mean[:, m, :],
-                in0=half_sums[:, m, 0:1],
-                scalar1=half_sums[:, m, 1:2],
-                scalar2=-1.0 / D,
-                op0=ALU.add,
-                op1=ALU.mult,
-            )
+        def square_sum(m, src, minus_mean, sum_sq):
             squares = acts.tile([P, D], BF16, tag="squares")
             nc.scalar.activation(
                 out=squares[:],
@@ -204,52 +201,100 @@ def tile_transformerblock_pa_kernel(
             nc.gpsimd.tensor_tensor(out=rstd[:], in0=var_eps[:], in1=minus_half[:], op=ALU.pow)
             return rstd
 
-        def centre_times_gain(dest, src, minus_mean, gain):
-            nc.vector.scalar_tensor_tensor(
-                out=dest[:], in0=src[:], scalar=minus_mean, in1=gain[:], op0=ALU.add, op1=ALU.mult
-            )
+        staged = {}
 
+        def empty_bank(c, m, n):
+            w, first_col = chunks[c]
+            out, bias = (out_1, b1_all) if w is W1 else (out_2, b2_all)
+            if (c, m) not in staged:
+                out_rows = staged_pool.tile([P, CHUNK], F32, tag="staged")
+                staged[(c, m)] = out_rows
+            nc.vector.tensor_tensor(
+                out=staged[(c, m)][:, n * BANK : (n + 1) * BANK],
+                in0=banks[(c, m, n)][:],
+                in1=bias[:, first_col + n * BANK : first_col + (n + 1) * BANK],
+                op=ALU.add,
+            )
+            if n == CHUNK // BANK - 1:
+                nc.sync.dma_start(
+                    out=out.flatten_outer_dims()[m * P : (m + 1) * P, first_col : first_col + CHUNK],
+                    in_=staged[(c, m)][:],
+                )
+
+        x_sb = consts.tile([P, TOKEN_TILES, D], BF16)
+        nc.sync.dma_start(out=x_sb[:], in_=x.flatten_outer_dims().rearrange("(m p) d -> p m d", p=P))
+        vec_rows = consts.tile([P, BANK], BF16)
+        nc.gpsimd.memset(vec_rows[:], 0.0)
+        first_row = {}
+        next_row = 0
+        for key, vec in (("bo", bo), ("ln2_g", ln2_g), ("ln2_b", ln2_b), ("fln_g", fln_g), ("fln_b", fln_b), ("b1", b1), ("b2", b2)):
+            n_rows = vec.shape[0] // BANK
+            nc.sync.dma_start(
+                out=vec_rows[next_row : next_row + n_rows, :], in_=vec.rearrange("(r c) -> r c", c=BANK)
+            )
+            first_row[key] = next_row
+            next_row += n_rows
         ident = consts.tile([P, P], BF16)
         make_identity(nc, ident[:])
+        ident_words = consts.tile([P, P], F32)
+        make_identity(nc, ident_words[:])
         minus_half = consts.tile([P, TOKEN_TILES, 1], F32)
-        nc.vector.memset(minus_half[:], -0.5)
-
-        norm_rows, norm_first = load_as_rows("norm", (bo, ln2_g, ln2_b, fln_g, fln_b))
+        nc.gpsimd.memset(minus_half[:], -0.5)
         h_sb = consts.tile([P, TOKEN_TILES, D], BF16)
         nc.sync.dma_start(
             out=h_sb[:], in_=h_attn.flatten_outer_dims().rearrange("(m p) d -> p m d", p=P)
         )
-        x_sb = consts.tile([P, TOKEN_TILES, D], BF16)
-        nc.sync.dma_start(out=x_sb[:], in_=x.flatten_outer_dims().rearrange("(m p) d -> p m d", p=P))
-        for u in range(PASSES):
-            load(u)
-        bias_rows, bias_first = load_as_rows("bias", (b1, b2))
-        for u in range(PASSES, RAW_BUFS):
-            load(u)
+        for i in range(RAW_BUFS):
+            load_next()
 
-        bo_all = spread("bo", norm_rows, norm_first[0], D, nc.vector.tensor_copy)
+        b1_all = consts.tile([P, F], BF16)
+        b2_all = consts.tile([P, F], BF16)
+
+        def spread_bias(key, pair, copy_out):
+            everywhere = b1_all if key == "b1" else b2_all
+            bank = spread(first_row[key] + 2 * pair, "even")
+            copy_out(out=everywhere[:, pair * 2 * BANK : (pair + 1) * 2 * BANK], in_=bank[:])
+
+        bo_bank = spread(first_row["bo"], "even")
         x_plus_bo = []
         for m in range(TOKEN_TILES):
             sum_row = rows.tile([P, D], F32, tag="row")
-            nc.vector.tensor_tensor(out=sum_row[:], in0=x_sb[:, m, :], in1=bo_all[:], op=ALU.add)
+            nc.vector.tensor_tensor(out=sum_row[:], in0=x_sb[:, m, :], in1=bo_bank[:], op=ALU.add)
             x_plus_bo.append(sum_row)
-        h_grouped = [flip_tokens(h_sb[:, m, :]) for m in range(TOKEN_TILES)]
-        h_q = [quantise_tokens("h%d" % m, h_grouped[m]) for m in range(TOKEN_TILES)]
-        ln2_g_all = spread("ln2_g", norm_rows, norm_first[1], D, nc.scalar.copy)
-        regroup(0, TOGETHER_COLS)
-        ln2_b_all = spread("ln2_b", norm_rows, norm_first[2], D, nc.scalar.copy)
-        quantise(0)
-        multiply(0, h_q)
-        regroup(1, TOGETHER_COLS)
-        quantise(1)
-        multiply(1, h_q)
+        spread_bias("b1", 0, nc.scalar.copy)
+        h_flipped = [flip_tokens(h_sb[:, m, :]) for m in range(TOKEN_TILES)]
+        h_grouped = [group_tokens(h_flipped[m]) for m in range(TOKEN_TILES)]
+        ln2_g_bank = spread(first_row["ln2_g"], "odd")
+        ln2_b_bank = spread(first_row["ln2_b"], "odd")
+        fln_g_bank = spread(first_row["fln_g"], "odd")
+        fln_b_bank = spread(first_row["fln_b"], "odd")
 
-        regroup(2, 0)
-        half_sums, minus_mean, sum_sq = new_statistics()
+        regroup("vector", 0, "A", 0, 672)
+        regroup("scalar", 0, "A", 672, CHUNK)
+        h_q = [quantise_tokens("h%d" % m, h_grouped[m]) for m in range(TOKEN_TILES)]
+        quantise(0, "A")
+        multiply(0, "A", h_q)
+        regroup("scalar", 0, "B", 176, BANK)
+        regroup("vector", 0, "B", 0, 176)
+        quantise(0, "B")
+        multiply(0, "B", h_q)
+        regroup("scalar", 0, "C", 184, BANK)
+        regroup("vector", 0, "C", 0, 184)
+        quantise(0, "C")
+        multiply(0, "C", h_q)
+        load_next()
+        load_next()
+
+        regroup("pool", 1, "C", 0, BANK)
+        regroup("scalar", 1, "A", 128, 512)
+        half_sums = small.tile([P, TOKEN_TILES, 2], F32, tag="half_sums")
+        scaled_halves = small.tile([P, TOKEN_TILES, 2], F32, tag="scaled_halves")
+        minus_mean = small.tile([P, TOKEN_TILES, 1], F32, tag="minus_mean")
+        sum_sq = small.tile([P, TOKEN_TILES, 1], F32, tag="sum_sq")
         r = []
         for m in range(TOKEN_TILES):
             r_row = rows.tile([P, D], F32, tag="row")
-            for n in range(UNIT_BANKS):
+            for n in range(D // BANK):
                 cols = slice(n * BANK, (n + 1) * BANK)
                 nc.vector.scalar_tensor_tensor(
                     out=r_row[:, cols],
@@ -260,78 +305,81 @@ def tile_transformerblock_pa_kernel(
                     op1=ALU.add,
                     accum_out=half_sums[:, m, n : n + 1],
                 )
-            measure(m, r_row, half_sums, minus_mean, sum_sq)
+            nc.scalar.activation(
+                out=scaled_halves[:, m, :],
+                in_=half_sums[:, m, :],
+                func=ACT.Copy,
+                scale=-1.0 / D,
+                accum_out=minus_mean[:, m, :],
+            )
+            square_sum(m, r_row, minus_mean, sum_sq)
             r.append(r_row)
         rstd = rstd_of(sum_sq)
-        fln_g_all = spread("fln_g", norm_rows, norm_first[3], D, nc.scalar.copy)
-        fln_b_all = spread("fln_b", norm_rows, norm_first[4], D, nc.scalar.copy)
+        regroup("pool", 1, "A", 512, CHUNK)
         for m in range(TOKEN_TILES):
-            centre_times_gain(r[m], r[m], minus_mean[:, m, :], ln2_g_all)
-        quantise(2)
-        b1_all = spread("b1", bias_rows, bias_first[0], F, nc.scalar.copy)
-        half_sums, minus_mean, sum_sq = new_statistics()
+            nc.vector.scalar_tensor_tensor(
+                out=r[m][:], in0=r[m][:], scalar=minus_mean[:, m, :], in1=ln2_g_bank[:], op0=ALU.add, op1=ALU.mult
+            )
+        for pair in range(1, 4):
+            spread_bias("b1", pair, nc.scalar.copy)
+        spread_bias("b2", 0, nc.scalar.copy)
+        row_sums = small.tile([P, TOKEN_TILES, 1], F32, tag="row_sums")
+        minus_mean_2 = small.tile([P, TOKEN_TILES, 1], F32, tag="minus_mean")
+        sum_sq_2 = small.tile([P, TOKEN_TILES, 1], F32, tag="sum_sq")
         for m in range(TOKEN_TILES):
-            for n in range(UNIT_BANKS):
-                cols = slice(n * BANK, (n + 1) * BANK)
-                nc.vector.scalar_tensor_tensor(
-                    out=r[m][:, cols],
-                    in0=r[m][:, cols],
-                    scalar=rstd[:, m, :],
-                    in1=ln2_b_all[:, cols],
-                    op0=ALU.mult,
-                    op1=ALU.add,
-                    accum_out=half_sums[:, m, n : n + 1],
-                )
+            nc.vector.scalar_tensor_tensor(
+                out=r[m][:],
+                in0=r[m][:],
+                scalar=rstd[:, m, :],
+                in1=ln2_b_bank[:],
+                op0=ALU.mult,
+                op1=ALU.add,
+                accum_out=row_sums[:, m, :],
+            )
             nc.sync.dma_start(out=r_out[m * P : (m + 1) * P, :], in_=r[m][:])
-            measure(m, r[m], half_sums, minus_mean, sum_sq)
-        rstd = rstd_of(sum_sq)
+            nc.scalar.activation(
+                out=minus_mean_2[:, m, :], in_=row_sums[:, m, :], func=ACT.Copy, scale=-1.0 / D
+            )
+            square_sum(m, r[m], minus_mean_2, sum_sq_2)
+        rstd_2 = rstd_of(sum_sq_2)
+        regroup("pool", 1, "B", 0, BANK)
         centred = []
         for m in range(TOKEN_TILES):
             centred_row = rows.tile([P, D], F32, tag="row")
-            centre_times_gain(centred_row, r[m], minus_mean[:, m, :], fln_g_all)
+            nc.vector.scalar_tensor_tensor(
+                out=centred_row[:], in0=r[m][:], scalar=minus_mean_2[:, m, :], in1=fln_g_bank[:], op0=ALU.add, op1=ALU.mult
+            )
             centred.append(centred_row)
-        regroup(3, 0)
-        h2_grouped = []
+        for pair in range(1, 4):
+            spread_bias("b2", pair, nc.scalar.copy)
+        h2_flipped = []
         for m in range(TOKEN_TILES):
             h2 = acts.tile([P, D], BF16, tag="h2")
             nc.vector.scalar_tensor_tensor(
-                out=h2[:],
-                in0=centred[m][:],
-                scalar=rstd[:, m, :],
-                in1=fln_b_all[:],
-                op0=ALU.mult,
-                op1=ALU.add,
+                out=h2[:], in0=centred[m][:], scalar=rstd_2[:, m, :], in1=fln_b_bank[:], op0=ALU.mult, op1=ALU.add
             )
-            h2_grouped.append(flip_tokens(h2))
-        b2_all = spread("b2", bias_rows, bias_first[1], F, nc.scalar.copy)
-        regroup(4, UNIT_COLS)
-        regroup(5, UNIT_COLS)
-        quantise(3)
+            h2_flipped.append(flip_tokens(h2[:]))
+        h2_grouped = [group_tokens(h2_flipped[m]) for m in range(TOKEN_TILES)]
+        regroup("vector", 1, "A", 0, 128)
+        regroup("vector", 2, "A", 0, VECTOR_COLS[2])
         h2_q = [quantise_tokens("h2_%d" % m, h2_grouped[m]) for m in range(TOKEN_TILES)]
+        load_next()
+        load_next()
 
-        def finish(chunk, m):
-            w, first_col, g = units[chunk * PASSES]
-            out, bias = (out_1, b1_all) if w is W1 else (out_2, b2_all)
-            staged = staged_pool.tile([P, UNIT_COLS], F32, tag="staged")
-            for n in range(UNIT_BANKS):
-                nc.vector.tensor_tensor(
-                    out=staged[:, n * BANK : (n + 1) * BANK],
-                    in0=banks[(chunk, m, n)][:],
-                    in1=bias[:, first_col + n * BANK : first_col + (n + 1) * BANK],
-                    op=ALU.add,
-                )
-            nc.sync.dma_start(
-                out=out.flatten_outer_dims()[m * P : (m + 1) * P, first_col : first_col + UNIT_COLS],
-                in_=staged[:],
-            )
-
-        for u in range(PASSES, 2 * PASSES):
-            multiply(u, h2_q)
-        for u in range(3 * PASSES, len(units) + LAG):
-            quantise(u - LAG)
-            multiply(u - LAG, h2_q)
-            if u < len(units):
-                regroup(u, STEADY_COLS)
-            finish((u - LAG - PASSES) // PASSES, u % TOKEN_TILES)
-        for m in range(TOKEN_TILES):
-            finish(last_chunk, m)
+        for c in range(1, last + 1):
+            if 2 < c + 1 <= last:
+                regroup("vector", c + 1, "A", 0, VECTOR_COLS[c + 1])
+            for piece in ("B", "A", "C"):
+                quantise(c, piece)
+                multiply(c, piece, h2_q)
+            if c + 2 <= last:
+                regroup("pool", c + 2, "C", 0, POOL_COLS[c + 2])
+            if c + 1 <= last:
+                regroup("scalar", c + 1, "B", 0, BANK)
+                regroup("scalar", c + 1, "A", VECTOR_COLS[c + 1], CHUNK)
+                regroup("scalar", c + 1, "C", POOL_COLS[c + 1], BANK)
+            for n in range(CHUNK // BANK):
+                for m in range(TOKEN_TILES):
+                    empty_bank(c, m, n)
+            load_next()
+            load_next()

@@ -24,8 +24,8 @@ CHUNK = 1024
 RAW_BUFS = 8
 RUN = 4
 EPS = 1e-5
-VECTOR_COLS = [0, 0, 416, 416, 416, 416, 416, 416, 416]
-POOL_COLS = [0, 512, 0, 400, 400, 400, 400, 400, 400]
+VECTOR_COLS = [0, 0, 320, 320, 320, 320, 320, 320, 320]
+POOL_COLS = [0, 512, 480, 480, 480, 480, 480, 480, 480]
 
 FLOPS = 2 * TOKENS * D * (D + 2 * F)
 
@@ -41,7 +41,7 @@ def tile_transformerblock_pa_kernel(
         for first_col in range(0, F, CHUNK):
             chunks.append((w, first_col))
     last = len(chunks) - 1
-    pieces = {"A": (0, 0, CHUNK), "B": (1, 0, BANK), "C": (1, BANK, BANK)}
+    pieces = {"A": (0, 0, CHUNK), "B": (1, 0, CHUNK)}
 
     with ExitStack() as ctx:
         consts = ctx.enter_context(tc.tile_pool(name="consts", bufs=1))
@@ -124,8 +124,8 @@ def tile_transformerblock_pa_kernel(
                 return
             g, first, width = pieces[piece]
             if (c, piece) not in grouped:
-                if piece == "C":
-                    slot = "C%d" % (1 if c == 0 else c % 2)
+                if piece == "B":
+                    slot = "B%d" % (1 if c == 0 else c % 2)
                     side_by_side = grouped_pool.tile([P, width, PACK], BF16, tag=slot, bufs=1, align_bytes=64)
                 else:
                     side_by_side = grouped_pool.tile([P, width, PACK], BF16, tag=piece, align_bytes=64)
@@ -165,8 +165,8 @@ def tile_transformerblock_pa_kernel(
         def multiply(c, piece, tokens_q):
             g, first, width = pieces[piece]
             codes, scales = packed[c]
-            for n in range(first // BANK, (first + width) // BANK):
-                for m in range(TOKEN_TILES):
+            for m in range(TOKEN_TILES):
+                for n in range(CHUNK // BANK):
                     opened = (c, m, n) in banks
                     if not opened:
                         acc = psum.tile([P, BANK], F32, tag=("odd" if c % 2 == 0 and c > 0 else "even"))
@@ -192,14 +192,12 @@ def tile_transformerblock_pa_kernel(
                 accum_out=sum_sq[:, m, :],
             )
 
-        def rstd_of(sum_sq):
-            var_eps = small.tile([P, TOKEN_TILES, 1], F32, tag="var_eps")
+        def rstd_of(m, sum_sq, rstd):
+            var_eps = small.tile([P, 1], F32, tag="var_eps")
             nc.gpsimd.tensor_scalar(
-                out=var_eps[:], in0=sum_sq[:], scalar1=1.0 / D, scalar2=EPS, op0=ALU.mult, op1=ALU.add
+                out=var_eps[:], in0=sum_sq[:, m, :], scalar1=1.0 / D, scalar2=EPS, op0=ALU.mult, op1=ALU.add
             )
-            rstd = small.tile([P, TOKEN_TILES, 1], F32, tag="rstd")
-            nc.gpsimd.tensor_tensor(out=rstd[:], in0=var_eps[:], in1=minus_half[:], op=ALU.pow)
-            return rstd
+            nc.gpsimd.tensor_tensor(out=rstd[:, m, :], in0=var_eps[:], in1=minus_half[:], op=ALU.pow)
 
         staged = {}
 
@@ -207,19 +205,22 @@ def tile_transformerblock_pa_kernel(
             w, first_col = chunks[c]
             out, bias = (out_1, b1_all) if w is W1 else (out_2, b2_all)
             if (c, m) not in staged:
-                out_rows = staged_pool.tile([P, CHUNK], F32, tag="staged")
-                staged[(c, m)] = out_rows
+                sums_and_bias = staged_pool.tile([P, CHUNK], F32, tag="staged")
+                staged[(c, m)] = sums_and_bias
             nc.vector.tensor_tensor(
                 out=staged[(c, m)][:, n * BANK : (n + 1) * BANK],
                 in0=banks[(c, m, n)][:],
                 in1=bias[:, first_col + n * BANK : first_col + (n + 1) * BANK],
                 op=ALU.add,
             )
-            if n == CHUNK // BANK - 1:
+            out_rows = out.flatten_outer_dims()[m * P : (m + 1) * P, :]
+            if c == last:
                 nc.sync.dma_start(
-                    out=out.flatten_outer_dims()[m * P : (m + 1) * P, first_col : first_col + CHUNK],
-                    in_=staged[(c, m)][:],
+                    out=out_rows[:, first_col + n * BANK : first_col + (n + 1) * BANK],
+                    in_=staged[(c, m)][:, n * BANK : (n + 1) * BANK],
                 )
+            elif n == CHUNK // BANK - 1:
+                nc.sync.dma_start(out=out_rows[:, first_col : first_col + CHUNK], in_=staged[(c, m)][:])
 
         x_sb = consts.tile([P, TOKEN_TILES, D], BF16)
         nc.sync.dma_start(out=x_sb[:], in_=x.flatten_outer_dims().rearrange("(m p) d -> p m d", p=P))
@@ -238,7 +239,7 @@ def tile_transformerblock_pa_kernel(
         make_identity(nc, ident[:])
         ident_words = consts.tile([P, P], F32)
         make_identity(nc, ident_words[:])
-        minus_half = consts.tile([P, TOKEN_TILES, 1], F32)
+        minus_half = consts.tile([P, 1], F32)
         nc.gpsimd.memset(minus_half[:], -0.5)
         h_sb = consts.tile([P, TOKEN_TILES, D], BF16)
         nc.sync.dma_start(
@@ -274,23 +275,20 @@ def tile_transformerblock_pa_kernel(
         h_q = [quantise_tokens("h%d" % m, h_grouped[m]) for m in range(TOKEN_TILES)]
         quantise(0, "A")
         multiply(0, "A", h_q)
-        regroup("scalar", 0, "B", 176, BANK)
-        regroup("vector", 0, "B", 0, 176)
+        regroup("scalar", 0, "B", 432, CHUNK)
+        regroup("vector", 0, "B", 0, 432)
         quantise(0, "B")
         multiply(0, "B", h_q)
-        regroup("scalar", 0, "C", 184, BANK)
-        regroup("vector", 0, "C", 0, 184)
-        quantise(0, "C")
-        multiply(0, "C", h_q)
         load_next()
         load_next()
 
-        regroup("pool", 1, "C", 0, BANK)
+        regroup("pool", 1, "B", BANK, CHUNK)
         regroup("scalar", 1, "A", 128, 512)
         half_sums = small.tile([P, TOKEN_TILES, 2], F32, tag="half_sums")
         scaled_halves = small.tile([P, TOKEN_TILES, 2], F32, tag="scaled_halves")
         minus_mean = small.tile([P, TOKEN_TILES, 1], F32, tag="minus_mean")
         sum_sq = small.tile([P, TOKEN_TILES, 1], F32, tag="sum_sq")
+        rstd = small.tile([P, TOKEN_TILES, 1], F32, tag="rstd")
         r = []
         for m in range(TOKEN_TILES):
             r_row = rows.tile([P, D], F32, tag="row")
@@ -313,8 +311,8 @@ def tile_transformerblock_pa_kernel(
                 accum_out=minus_mean[:, m, :],
             )
             square_sum(m, r_row, minus_mean, sum_sq)
+            rstd_of(m, sum_sq, rstd)
             r.append(r_row)
-        rstd = rstd_of(sum_sq)
         regroup("pool", 1, "A", 512, CHUNK)
         for m in range(TOKEN_TILES):
             nc.vector.scalar_tensor_tensor(
@@ -322,10 +320,10 @@ def tile_transformerblock_pa_kernel(
             )
         for pair in range(1, 4):
             spread_bias("b1", pair, nc.scalar.copy)
-        spread_bias("b2", 0, nc.scalar.copy)
         row_sums = small.tile([P, TOKEN_TILES, 1], F32, tag="row_sums")
         minus_mean_2 = small.tile([P, TOKEN_TILES, 1], F32, tag="minus_mean")
         sum_sq_2 = small.tile([P, TOKEN_TILES, 1], F32, tag="sum_sq")
+        rstd_2 = small.tile([P, TOKEN_TILES, 1], F32, tag="rstd")
         for m in range(TOKEN_TILES):
             nc.vector.scalar_tensor_tensor(
                 out=r[m][:],
@@ -341,8 +339,8 @@ def tile_transformerblock_pa_kernel(
                 out=minus_mean_2[:, m, :], in_=row_sums[:, m, :], func=ACT.Copy, scale=-1.0 / D
             )
             square_sum(m, r[m], minus_mean_2, sum_sq_2)
-        rstd_2 = rstd_of(sum_sq_2)
-        regroup("pool", 1, "B", 0, BANK)
+            rstd_of(m, sum_sq_2, rstd_2)
+        regroup("pool", 2, "B", CHUNK - POOL_COLS[2], CHUNK)
         centred = []
         for m in range(TOKEN_TILES):
             centred_row = rows.tile([P, D], F32, tag="row")
@@ -350,8 +348,7 @@ def tile_transformerblock_pa_kernel(
                 out=centred_row[:], in0=r[m][:], scalar=minus_mean_2[:, m, :], in1=fln_g_bank[:], op0=ALU.add, op1=ALU.mult
             )
             centred.append(centred_row)
-        for pair in range(1, 4):
-            spread_bias("b2", pair, nc.scalar.copy)
+        regroup("scalar", 1, "B", 64, BANK)
         h2_flipped = []
         for m in range(TOKEN_TILES):
             h2 = acts.tile([P, D], BF16, tag="h2")
@@ -361,25 +358,29 @@ def tile_transformerblock_pa_kernel(
             h2_flipped.append(flip_tokens(h2[:]))
         h2_grouped = [group_tokens(h2_flipped[m]) for m in range(TOKEN_TILES)]
         regroup("vector", 1, "A", 0, 128)
+        regroup("vector", 1, "B", 0, 64)
         regroup("vector", 2, "A", 0, VECTOR_COLS[2])
         h2_q = [quantise_tokens("h2_%d" % m, h2_grouped[m]) for m in range(TOKEN_TILES)]
         load_next()
         load_next()
 
-        for c in range(1, last + 1):
+        for c in range(1, last + 2):
             if 2 < c + 1 <= last:
                 regroup("vector", c + 1, "A", 0, VECTOR_COLS[c + 1])
-            for piece in ("B", "A", "C"):
-                quantise(c, piece)
-                multiply(c, piece, h2_q)
+            if c <= last:
+                for piece in ("A", "B"):
+                    quantise(c, piece)
+                    multiply(c, piece, h2_q)
             if c + 2 <= last:
-                regroup("pool", c + 2, "C", 0, POOL_COLS[c + 2])
+                regroup("pool", c + 2, "B", CHUNK - POOL_COLS[c + 2], CHUNK)
             if c + 1 <= last:
-                regroup("scalar", c + 1, "B", 0, BANK)
                 regroup("scalar", c + 1, "A", VECTOR_COLS[c + 1], CHUNK)
-                regroup("scalar", c + 1, "C", POOL_COLS[c + 1], BANK)
-            for n in range(CHUNK // BANK):
-                for m in range(TOKEN_TILES):
-                    empty_bank(c, m, n)
+                regroup("scalar", c + 1, "B", 0, CHUNK - POOL_COLS[c + 1])
+            if c <= 4:
+                spread_bias("b2", c - 1, nc.scalar.copy)
+            for cc, m in ((c - 1, 1), (c, 0)):
+                if 1 <= cc <= last:
+                    for n in range(CHUNK // BANK):
+                        empty_bank(cc, m, n)
             load_next()
             load_next()

@@ -24,7 +24,7 @@ CHUNK = 1024
 RAW_BUFS = 8
 RUN = 4
 EPS = 1e-5
-VECTOR_COLS = [0, 0, 320, 320, 320, 320, 320, 320, 320]
+VECTOR_COLS = [0, 0, 256, 256, 256, 256, 256, 256, 256]
 POOL_COLS = [0, 512, 480, 480, 480, 480, 480, 480, 480]
 
 FLOPS = 2 * TOKENS * D * (D + 2 * F)
@@ -228,7 +228,7 @@ def tile_transformerblock_pa_kernel(
         nc.gpsimd.memset(vec_rows[:], 0.0)
         first_row = {}
         next_row = 0
-        for key, vec in (("bo", bo), ("ln2_g", ln2_g), ("ln2_b", ln2_b), ("fln_g", fln_g), ("fln_b", fln_b), ("b1", b1), ("b2", b2)):
+        for key, vec in (("bo", bo), ("ln2_g", ln2_g), ("ln2_b", ln2_b), ("fln_g", fln_g), ("fln_b", fln_b)):
             n_rows = vec.shape[0] // BANK
             nc.sync.dma_start(
                 out=vec_rows[next_row : next_row + n_rows, :], in_=vec.rearrange("(r c) -> r c", c=BANK)
@@ -249,12 +249,8 @@ def tile_transformerblock_pa_kernel(
             load_next()
 
         b1_all = consts.tile([P, F], BF16)
+        nc.sync.dma_start(out=b1_all[:], in_=b1.partition_broadcast(P))
         b2_all = consts.tile([P, F], BF16)
-
-        def spread_bias(key, pair, copy_out):
-            everywhere = b1_all if key == "b1" else b2_all
-            bank = spread(first_row[key] + 2 * pair, "even")
-            copy_out(out=everywhere[:, pair * 2 * BANK : (pair + 1) * 2 * BANK], in_=bank[:])
 
         bo_bank = spread(first_row["bo"], "even")
         x_plus_bo = []
@@ -262,7 +258,6 @@ def tile_transformerblock_pa_kernel(
             sum_row = rows.tile([P, D], F32, tag="row")
             nc.vector.tensor_tensor(out=sum_row[:], in0=x_sb[:, m, :], in1=bo_bank[:], op=ALU.add)
             x_plus_bo.append(sum_row)
-        spread_bias("b1", 0, nc.scalar.copy)
         h_flipped = [flip_tokens(h_sb[:, m, :]) for m in range(TOKEN_TILES)]
         h_grouped = [group_tokens(h_flipped[m]) for m in range(TOKEN_TILES)]
         ln2_g_bank = spread(first_row["ln2_g"], "odd")
@@ -281,6 +276,7 @@ def tile_transformerblock_pa_kernel(
         multiply(0, "B", h_q)
         load_next()
         load_next()
+        nc.sync.dma_start(out=b2_all[:], in_=b2.partition_broadcast(P))
 
         regroup("pool", 1, "B", BANK, CHUNK)
         regroup("scalar", 1, "A", 128, 512)
@@ -318,8 +314,7 @@ def tile_transformerblock_pa_kernel(
             nc.vector.scalar_tensor_tensor(
                 out=r[m][:], in0=r[m][:], scalar=minus_mean[:, m, :], in1=ln2_g_bank[:], op0=ALU.add, op1=ALU.mult
             )
-        for pair in range(1, 4):
-            spread_bias("b1", pair, nc.scalar.copy)
+        regroup("scalar", 1, "B", 0, BANK)
         row_sums = small.tile([P, TOKEN_TILES, 1], F32, tag="row_sums")
         minus_mean_2 = small.tile([P, TOKEN_TILES, 1], F32, tag="minus_mean")
         sum_sq_2 = small.tile([P, TOKEN_TILES, 1], F32, tag="sum_sq")
@@ -348,7 +343,7 @@ def tile_transformerblock_pa_kernel(
                 out=centred_row[:], in0=r[m][:], scalar=minus_mean_2[:, m, :], in1=fln_g_bank[:], op0=ALU.add, op1=ALU.mult
             )
             centred.append(centred_row)
-        regroup("scalar", 1, "B", 64, BANK)
+        regroup("scalar", 2, "A", VECTOR_COLS[2], 768)
         h2_flipped = []
         for m in range(TOKEN_TILES):
             h2 = acts.tile([P, D], BF16, tag="h2")
@@ -358,26 +353,26 @@ def tile_transformerblock_pa_kernel(
             h2_flipped.append(flip_tokens(h2[:]))
         h2_grouped = [group_tokens(h2_flipped[m]) for m in range(TOKEN_TILES)]
         regroup("vector", 1, "A", 0, 128)
-        regroup("vector", 1, "B", 0, 64)
+        regroup("vector", 1, "B", 0, 0)
         regroup("vector", 2, "A", 0, VECTOR_COLS[2])
         h2_q = [quantise_tokens("h2_%d" % m, h2_grouped[m]) for m in range(TOKEN_TILES)]
         load_next()
         load_next()
 
         for c in range(1, last + 2):
-            if 2 < c + 1 <= last:
+            if 3 < c + 1 <= last:
                 regroup("vector", c + 1, "A", 0, VECTOR_COLS[c + 1])
             if c <= last:
                 for piece in ("A", "B"):
                     quantise(c, piece)
                     multiply(c, piece, h2_q)
+            if c == 1:
+                regroup("vector", 3, "A", 0, VECTOR_COLS[3])
             if c + 2 <= last:
                 regroup("pool", c + 2, "B", CHUNK - POOL_COLS[c + 2], CHUNK)
             if c + 1 <= last:
-                regroup("scalar", c + 1, "A", VECTOR_COLS[c + 1], CHUNK)
+                regroup("scalar", c + 1, "A", 768 if c + 1 == 2 else VECTOR_COLS[c + 1], CHUNK)
                 regroup("scalar", c + 1, "B", 0, CHUNK - POOL_COLS[c + 1])
-            if c <= 4:
-                spread_bias("b2", c - 1, nc.scalar.copy)
             for cc, m in ((c - 1, 1), (c, 0)):
                 if 1 <= cc <= last:
                     for n in range(CHUNK // BANK):

@@ -162,25 +162,32 @@ def tile_transformerblock_pa_kernel(
                 in_=grouped[(c, piece)][:].rearrange("p n t -> p (n t)"),
             )
 
-        def multiply(c, piece, tokens_q):
+        def multiply(c, piece, m, tokens_q):
             g, first, width = pieces[piece]
             codes, scales = packed[c]
-            for m in range(TOKEN_TILES):
-                for n in range(CHUNK // BANK):
-                    opened = (c, m, n) in banks
-                    if not opened:
-                        acc = psum.tile([P, BANK], F32, tag=("odd" if c % 2 == 0 and c > 0 else "even"))
-                        banks[(c, m, n)] = acc
-                    token_codes, token_scales = tokens_q[m]
-                    nc.tensor.matmul_mx(
-                        out=banks[(c, m, n)][:],
-                        lhsT=token_codes[:, g * P : (g + 1) * P].bitcast(FP8X4),
-                        lhsT_scale=token_scales[:, g * P : (g + 1) * P],
-                        rhs=codes[:, g, n * BANK : (n + 1) * BANK].bitcast(FP8X4),
-                        rhs_scale=scales[:, g, n * BANK : (n + 1) * BANK],
-                        start=not opened,
-                        stop=opened,
-                    )
+            token_codes, token_scales = tokens_q[m]
+            for n in range(CHUNK // BANK):
+                opened = (c, m, n) in banks
+                if not opened:
+                    acc = psum.tile([P, BANK], F32, tag=("odd" if c % 2 == 0 and c > 0 else "even"))
+                    banks[(c, m, n)] = acc
+                nc.tensor.matmul_mx(
+                    out=banks[(c, m, n)][:],
+                    lhsT=token_codes[:, g * P : (g + 1) * P].bitcast(FP8X4),
+                    lhsT_scale=token_scales[:, g * P : (g + 1) * P],
+                    rhs=codes[:, g, n * BANK : (n + 1) * BANK].bitcast(FP8X4),
+                    rhs_scale=scales[:, g, n * BANK : (n + 1) * BANK],
+                    start=not opened,
+                    stop=opened,
+                )
+
+        def quantise_and_multiply(c, tokens_q):
+            quantise(c, "A")
+            multiply(c, "A", 0, tokens_q)
+            quantise(c, "B")
+            multiply(c, "B", 0, tokens_q)
+            multiply(c, "A", 1, tokens_q)
+            multiply(c, "B", 1, tokens_q)
 
         def square_sum(m, src, minus_mean, sum_sq):
             squares = acts.tile([P, D], BF16, tag="squares")
@@ -193,11 +200,13 @@ def tile_transformerblock_pa_kernel(
             )
 
         def rstd_of(m, sum_sq, rstd):
-            var_eps = small.tile([P, 1], F32, tag="var_eps")
-            nc.gpsimd.tensor_scalar(
-                out=var_eps[:], in0=sum_sq[:, m, :], scalar1=1.0 / D, scalar2=EPS, op0=ALU.mult, op1=ALU.add
+            nc.scalar.activation(
+                out=rstd[:, m, :],
+                in_=sum_sq[:, m, :],
+                func=ACT.Abs_reciprocal_sqrt,
+                scale=1.0 / D,
+                bias=eps_column[:],
             )
-            nc.gpsimd.tensor_tensor(out=rstd[:, m, :], in0=var_eps[:], in1=minus_half[:], op=ALU.pow)
 
         staged = {}
 
@@ -239,8 +248,10 @@ def tile_transformerblock_pa_kernel(
         make_identity(nc, ident[:])
         ident_words = consts.tile([P, P], F32)
         make_identity(nc, ident_words[:])
-        minus_half = consts.tile([P, 1], F32)
-        nc.gpsimd.memset(minus_half[:], -0.5)
+        eps_column = consts.tile([P, 1], F32)
+        nc.gpsimd.memset(eps_column[:], EPS)
+        warm = consts.tile([P, 1], F32)
+        nc.scalar.activation(out=warm[:], in_=eps_column[:], func=ACT.Abs_reciprocal_sqrt)
         h_sb = consts.tile([P, TOKEN_TILES, D], BF16)
         nc.sync.dma_start(
             out=h_sb[:], in_=h_attn.flatten_outer_dims().rearrange("(m p) d -> p m d", p=P)
@@ -269,11 +280,13 @@ def tile_transformerblock_pa_kernel(
         regroup("scalar", 0, "A", 672, CHUNK)
         h_q = [quantise_tokens("h%d" % m, h_grouped[m]) for m in range(TOKEN_TILES)]
         quantise(0, "A")
-        multiply(0, "A", h_q)
+        multiply(0, "A", 0, h_q)
         regroup("scalar", 0, "B", 432, CHUNK)
         regroup("vector", 0, "B", 0, 432)
         quantise(0, "B")
-        multiply(0, "B", h_q)
+        multiply(0, "B", 0, h_q)
+        multiply(0, "A", 1, h_q)
+        multiply(0, "B", 1, h_q)
         load_next()
         load_next()
         nc.sync.dma_start(out=b2_all[:], in_=b2.partition_broadcast(P))
@@ -363,9 +376,7 @@ def tile_transformerblock_pa_kernel(
             if 3 < c + 1 <= last:
                 regroup("vector", c + 1, "A", 0, VECTOR_COLS[c + 1])
             if c <= last:
-                for piece in ("A", "B"):
-                    quantise(c, piece)
-                    multiply(c, piece, h2_q)
+                quantise_and_multiply(c, h2_q)
             if c == 1:
                 regroup("vector", 3, "A", 0, VECTOR_COLS[3])
             if c + 2 <= last:

@@ -21,7 +21,9 @@ F = 4096
 PASSES = D // K_PASS
 BANK = 512
 CHUNK = 1024
-RAW_BUFS = 8
+LOAD_COLS = 2048
+RAW_BUFS = 6
+ROW_BUFS = 8
 RUN = 4
 EPS = 1e-5
 VECTOR_COLS = [0, 0, 256, 256, 256, 256, 256, 256, 256]
@@ -41,17 +43,21 @@ def tile_transformerblock_pa_kernel(
         for first_col in range(0, F, CHUNK):
             chunks.append((w, first_col))
     last = len(chunks) - 1
+    loads = []
+    for w in (W1, W2):
+        for first_col in range(0, F, LOAD_COLS):
+            for g in range(PASSES):
+                loads.append((w, first_col, g))
     pieces = {"A": (0, 0, CHUNK), "B": (1, 0, CHUNK)}
 
     with ExitStack() as ctx:
         consts = ctx.enter_context(tc.tile_pool(name="consts", bufs=1))
         small = ctx.enter_context(tc.tile_pool(name="small", bufs=2))
-        rows = ctx.enter_context(tc.tile_pool(name="rows", bufs=4))
+        rows = ctx.enter_context(tc.tile_pool(name="rows", bufs=ROW_BUFS))
         acts = ctx.enter_context(tc.tile_pool(name="acts", bufs=2))
         raw_pool = ctx.enter_context(tc.tile_pool(name="raw", bufs=RAW_BUFS))
         grouped_pool = ctx.enter_context(tc.tile_pool(name="grouped", bufs=2))
-        quantised = ctx.enter_context(tc.tile_pool(name="quantised", bufs=4))
-        staged_pool = ctx.enter_context(tc.tile_pool(name="staged", bufs=4))
+        quantised = ctx.enter_context(tc.tile_pool(name="quantised", bufs=3))
         psum = ctx.enter_context(tc.psum_pool(name="psum", bufs=4))
         ctx.enter_context(tc.manual_schedule())
 
@@ -62,19 +68,20 @@ def tile_transformerblock_pa_kernel(
         loaded = []
 
         def load_next():
-            c, g = divmod(len(loaded), PASSES)
-            if c > last:
+            if len(loaded) == len(loads):
                 return
-            w, first_col = chunks[c]
-            rows_of_pass = raw_pool.tile([P, PACK, CHUNK], BF16, tag="raw")
+            w, first_col, g = loads[len(loaded)]
+            rows_of_pass = raw_pool.tile([P, PACK, LOAD_COLS], BF16, tag="raw")
             nc.sync.dma_start(
                 out=rows_of_pass[:],
-                in_=w[g * K_PASS : (g + 1) * K_PASS, first_col : first_col + CHUNK].rearrange(
+                in_=w[g * K_PASS : (g + 1) * K_PASS, first_col : first_col + LOAD_COLS].rearrange(
                     "(p t) n -> p t n", p=P
                 ),
             )
-            raw[(c, g)] = rows_of_pass
-            loaded.append((c, g))
+            for c in range(1, last + 1):
+                if chunks[c][0] is w and first_col <= chunks[c][1] < first_col + LOAD_COLS:
+                    raw[(c, g)] = rows_of_pass[:, :, chunks[c][1] - first_col : chunks[c][1] - first_col + CHUNK]
+            loaded.append((w, first_col, g))
 
         def spread(first, tag):
             bank = psum.tile([P, 2 * BANK], BF16, tag=tag)
@@ -124,11 +131,10 @@ def tile_transformerblock_pa_kernel(
                 return
             g, first, width = pieces[piece]
             if (c, piece) not in grouped:
-                if piece == "B":
-                    slot = "B%d" % (1 if c == 0 else c % 2)
-                    side_by_side = grouped_pool.tile([P, width, PACK], BF16, tag=slot, bufs=1, align_bytes=64)
-                else:
-                    side_by_side = grouped_pool.tile([P, width, PACK], BF16, tag=piece, align_bytes=64)
+                slot = piece + str(c % 2)
+                if c == 0:
+                    slot = "B1" if piece == "A" else "A1"
+                side_by_side = grouped_pool.tile([P, width, PACK], BF16, tag=slot, bufs=1, align_bytes=64)
                 grouped[(c, piece)] = side_by_side
             dst = grouped[(c, piece)][:, lo:hi, :]
             src = raw[(c, g)][:, :, first + lo : first + hi]
@@ -214,7 +220,7 @@ def tile_transformerblock_pa_kernel(
             w, first_col = chunks[c]
             out, bias = (out_1, b1_all) if w is W1 else (out_2, b2_all)
             if (c, m) not in staged:
-                sums_and_bias = staged_pool.tile([P, CHUNK], F32, tag="staged")
+                sums_and_bias = rows.tile([P, CHUNK], F32, tag="row")
                 staged[(c, m)] = sums_and_bias
             nc.vector.tensor_tensor(
                 out=staged[(c, m)][:, n * BANK : (n + 1) * BANK],
@@ -231,7 +237,7 @@ def tile_transformerblock_pa_kernel(
             elif n == CHUNK // BANK - 1:
                 nc.sync.dma_start(out=out_rows[:, first_col : first_col + CHUNK], in_=staged[(c, m)][:])
 
-        x_sb = consts.tile([P, TOKEN_TILES, D], BF16)
+        x_sb = rows.tile([P, TOKEN_TILES, D], BF16, tag="row")
         nc.sync.dma_start(out=x_sb[:], in_=x.flatten_outer_dims().rearrange("(m p) d -> p m d", p=P))
         vec_rows = consts.tile([P, BANK], BF16)
         nc.gpsimd.memset(vec_rows[:], 0.0)
@@ -252,16 +258,23 @@ def tile_transformerblock_pa_kernel(
         nc.gpsimd.memset(eps_column[:], EPS)
         warm = consts.tile([P, 1], F32)
         nc.scalar.activation(out=warm[:], in_=eps_column[:], func=ACT.Abs_reciprocal_sqrt)
-        h_sb = consts.tile([P, TOKEN_TILES, D], BF16)
+        h_sb = rows.tile([P, TOKEN_TILES, D], BF16, tag="row")
         nc.sync.dma_start(
             out=h_sb[:], in_=h_attn.flatten_outer_dims().rearrange("(m p) d -> p m d", p=P)
         )
-        for i in range(RAW_BUFS):
-            load_next()
-
         b1_all = consts.tile([P, F], BF16)
-        nc.sync.dma_start(out=b1_all[:], in_=b1.partition_broadcast(P))
         b2_all = consts.tile([P, F], BF16)
+        wo_rows = raw_pool.tile([P, PASSES, PACK, CHUNK], BF16, tag="raw")
+        for g in range(PASSES):
+            nc.sync.dma_start(
+                out=wo_rows[:, g, :, :], in_=Wo[g * K_PASS : (g + 1) * K_PASS, :].rearrange("(p t) n -> p t n", p=P)
+            )
+            raw[(0, g)] = wo_rows[:, g, :, :]
+        for i in range(RAW_BUFS - 1):
+            load_next()
+            if i == 1:
+                nc.sync.dma_start(out=b1_all[:], in_=b1.partition_broadcast(P))
+
 
         bo_bank = spread(first_row["bo"], "even")
         x_plus_bo = []
@@ -288,11 +301,13 @@ def tile_transformerblock_pa_kernel(
         multiply(0, "A", 1, h_q)
         multiply(0, "B", 1, h_q)
         load_next()
-        load_next()
         nc.sync.dma_start(out=b2_all[:], in_=b2.partition_broadcast(P))
 
+        regroup("pool", 1, "A", BANK, CHUNK)
+        regroup("pool", 2, "A", BANK, CHUNK)
         regroup("pool", 1, "B", BANK, CHUNK)
-        regroup("scalar", 1, "A", 128, 512)
+        regroup("pool", 2, "B", CHUNK - POOL_COLS[2], CHUNK)
+        regroup("scalar", 1, "A", 128, BANK)
         half_sums = small.tile([P, TOKEN_TILES, 2], F32, tag="half_sums")
         scaled_halves = small.tile([P, TOKEN_TILES, 2], F32, tag="scaled_halves")
         minus_mean = small.tile([P, TOKEN_TILES, 1], F32, tag="minus_mean")
@@ -322,7 +337,6 @@ def tile_transformerblock_pa_kernel(
             square_sum(m, r_row, minus_mean, sum_sq)
             rstd_of(m, sum_sq, rstd)
             r.append(r_row)
-        regroup("pool", 1, "A", 512, CHUNK)
         for m in range(TOKEN_TILES):
             nc.vector.scalar_tensor_tensor(
                 out=r[m][:], in0=r[m][:], scalar=minus_mean[:, m, :], in1=ln2_g_bank[:], op0=ALU.add, op1=ALU.mult
@@ -348,7 +362,6 @@ def tile_transformerblock_pa_kernel(
             )
             square_sum(m, r[m], minus_mean_2, sum_sq_2)
             rstd_of(m, sum_sq_2, rstd_2)
-        regroup("pool", 2, "B", CHUNK - POOL_COLS[2], CHUNK)
         centred = []
         for m in range(TOKEN_TILES):
             centred_row = rows.tile([P, D], F32, tag="row")
@@ -356,7 +369,7 @@ def tile_transformerblock_pa_kernel(
                 out=centred_row[:], in0=r[m][:], scalar=minus_mean_2[:, m, :], in1=fln_g_bank[:], op0=ALU.add, op1=ALU.mult
             )
             centred.append(centred_row)
-        regroup("scalar", 2, "A", VECTOR_COLS[2], 768)
+        regroup("scalar", 2, "A", VECTOR_COLS[2], BANK)
         h2_flipped = []
         for m in range(TOKEN_TILES):
             h2 = acts.tile([P, D], BF16, tag="h2")
@@ -366,10 +379,8 @@ def tile_transformerblock_pa_kernel(
             h2_flipped.append(flip_tokens(h2[:]))
         h2_grouped = [group_tokens(h2_flipped[m]) for m in range(TOKEN_TILES)]
         regroup("vector", 1, "A", 0, 128)
-        regroup("vector", 1, "B", 0, 0)
         regroup("vector", 2, "A", 0, VECTOR_COLS[2])
         h2_q = [quantise_tokens("h2_%d" % m, h2_grouped[m]) for m in range(TOKEN_TILES)]
-        load_next()
         load_next()
 
         for c in range(1, last + 2):
@@ -382,11 +393,11 @@ def tile_transformerblock_pa_kernel(
             if c + 2 <= last:
                 regroup("pool", c + 2, "B", CHUNK - POOL_COLS[c + 2], CHUNK)
             if c + 1 <= last:
-                regroup("scalar", c + 1, "A", 768 if c + 1 == 2 else VECTOR_COLS[c + 1], CHUNK)
+                regroup("scalar", c + 1, "A", CHUNK if c + 1 == 2 else VECTOR_COLS[c + 1], CHUNK)
                 regroup("scalar", c + 1, "B", 0, CHUNK - POOL_COLS[c + 1])
             for cc, m in ((c - 1, 1), (c, 0)):
                 if 1 <= cc <= last:
                     for n in range(CHUNK // BANK):
                         empty_bank(cc, m, n)
-            load_next()
-            load_next()
+            if c % 2 == 1:
+                load_next()

@@ -188,7 +188,8 @@ def tile_transformerblock_pa_kernel(
                 )
 
         def quantise_and_multiply(c, tokens_q):
-            quantise(c, "A")
+            if c > 1:
+                quantise(c, "A")
             multiply(c, "A", 0, tokens_q)
             quantise(c, "B")
             multiply(c, "B", 0, tokens_q)
@@ -380,6 +381,7 @@ def tile_transformerblock_pa_kernel(
         h2_grouped = [group_tokens(h2_flipped[m]) for m in range(TOKEN_TILES)]
         regroup("vector", 1, "A", 0, 128)
         regroup("vector", 2, "A", 0, VECTOR_COLS[2])
+        quantise(1, "A")
         h2_q = [quantise_tokens("h2_%d" % m, h2_grouped[m]) for m in range(TOKEN_TILES)]
         load_next()
 

@@ -308,6 +308,7 @@ def tile_transformerblock_pa_kernel(
         regroup("pool", 2, "A", BANK, CHUNK)
         regroup("pool", 1, "B", BANK, CHUNK)
         regroup("pool", 2, "B", CHUNK - POOL_COLS[2], CHUNK)
+        regroup("pool", 2, "B", 224, CHUNK - POOL_COLS[2])
         regroup("scalar", 1, "A", 128, BANK)
         half_sums = small.tile([P, TOKEN_TILES, 2], F32, tag="half_sums")
         scaled_halves = small.tile([P, TOKEN_TILES, 2], F32, tag="scaled_halves")
@@ -371,6 +372,7 @@ def tile_transformerblock_pa_kernel(
             )
             centred.append(centred_row)
         regroup("scalar", 2, "A", VECTOR_COLS[2], BANK)
+        regroup("scalar", 2, "B", 0, 224)
         h2_flipped = []
         for m in range(TOKEN_TILES):
             h2 = acts.tile([P, D], BF16, tag="h2")
@@ -396,7 +398,8 @@ def tile_transformerblock_pa_kernel(
                 regroup("pool", c + 2, "B", CHUNK - POOL_COLS[c + 2], CHUNK)
             if c + 1 <= last:
                 regroup("scalar", c + 1, "A", CHUNK if c + 1 == 2 else VECTOR_COLS[c + 1], CHUNK)
-                regroup("scalar", c + 1, "B", 0, CHUNK - POOL_COLS[c + 1])
+                if c + 1 > 2:
+                    regroup("scalar", c + 1, "B", 0, CHUNK - POOL_COLS[c + 1])
             for cc, m in ((c - 1, 1), (c, 0)):
                 if 1 <= cc <= last:
                     for n in range(CHUNK // BANK):

@@ -302,7 +302,6 @@ def tile_transformerblock_pa_kernel(
         multiply(0, "A", 1, h_q)
         multiply(0, "B", 1, h_q)
         load_next()
-        nc.sync.dma_start(out=b2_all[:], in_=b2.partition_broadcast(P))
 
         regroup("pool", 1, "A", BANK, CHUNK)
         regroup("pool", 2, "A", BANK, CHUNK)
@@ -386,6 +385,8 @@ def tile_transformerblock_pa_kernel(
         quantise(1, "A")
         h2_q = [quantise_tokens("h2_%d" % m, h2_grouped[m]) for m in range(TOKEN_TILES)]
         load_next()
+        load_next()
+        nc.sync.dma_start(out=b2_all[:], in_=b2.partition_broadcast(P))
 
         for c in range(1, last + 2):
             if 3 < c + 1 <= last:
@@ -404,5 +405,3 @@ def tile_transformerblock_pa_kernel(
                 if 1 <= cc <= last:
                     for n in range(CHUNK // BANK):
                         empty_bank(cc, m, n)
-            if c % 2 == 1:
-                load_next()

@@ -96,6 +96,11 @@ def tile_transformerblock_pa_kernel(
                 )
             return bank
 
+        def spread_bias(key, bias, banks_of_bias):
+            for i in banks_of_bias:
+                bank = spread(first_row[key] + 2 * i, "odd")
+                nc.scalar.copy(out=bias[:, i * 2 * BANK : (i + 1) * 2 * BANK], in_=bank[:])
+
         def flip_tokens(token_rows):
             words = token_rows.bitcast(F32)
             flipped = psum.tile([P, PASSES * 2, P], F32, tag="even")
@@ -238,19 +243,24 @@ def tile_transformerblock_pa_kernel(
             elif n == CHUNK // BANK - 1:
                 nc.sync.dma_start(out=out_rows[:, first_col : first_col + CHUNK], in_=staged[(c, m)][:])
 
+        vec_rows = consts.tile([P, BANK], BF16)
+        nc.vector.memset(vec_rows[:], 0.0)
+        first_row = {}
+        filled = []
+
+        def load_vector(queue, key, vec):
+            row = len(filled)
+            n_rows = vec.shape[0] // BANK
+            queue.dma_start(out=vec_rows[row : row + n_rows, :], in_=vec.rearrange("(r c) -> r c", c=BANK))
+            first_row[key] = row
+            filled.extend(range(row, row + n_rows))
+
+        load_vector(nc.scalar, "bo", bo)
+        load_vector(nc.scalar, "b1", b1)
         x_sb = rows.tile([P, TOKEN_TILES, D], BF16, tag="row")
         nc.sync.dma_start(out=x_sb[:], in_=x.flatten_outer_dims().rearrange("(m p) d -> p m d", p=P))
-        vec_rows = consts.tile([P, BANK], BF16)
-        nc.gpsimd.memset(vec_rows[:], 0.0)
-        first_row = {}
-        next_row = 0
-        for key, vec in (("bo", bo), ("ln2_g", ln2_g), ("ln2_b", ln2_b), ("fln_g", fln_g), ("fln_b", fln_b)):
-            n_rows = vec.shape[0] // BANK
-            nc.sync.dma_start(
-                out=vec_rows[next_row : next_row + n_rows, :], in_=vec.rearrange("(r c) -> r c", c=BANK)
-            )
-            first_row[key] = next_row
-            next_row += n_rows
+        for key, vec in (("ln2_g", ln2_g), ("ln2_b", ln2_b), ("fln_g", fln_g), ("fln_b", fln_b)):
+            load_vector(nc.sync, key, vec)
         ident = consts.tile([P, P], BF16)
         make_identity(nc, ident[:])
         ident_words = consts.tile([P, P], F32)
@@ -271,11 +281,9 @@ def tile_transformerblock_pa_kernel(
                 out=wo_rows[:, g, :, :], in_=Wo[g * K_PASS : (g + 1) * K_PASS, :].rearrange("(p t) n -> p t n", p=P)
             )
             raw[(0, g)] = wo_rows[:, g, :, :]
+        load_vector(nc.sync, "b2", b2)
         for i in range(RAW_BUFS - 1):
             load_next()
-            if i == 1:
-                nc.sync.dma_start(out=b1_all[:], in_=b1.partition_broadcast(P))
-
 
         bo_bank = spread(first_row["bo"], "even")
         x_plus_bo = []
@@ -283,8 +291,10 @@ def tile_transformerblock_pa_kernel(
             sum_row = rows.tile([P, D], F32, tag="row")
             nc.vector.tensor_tensor(out=sum_row[:], in0=x_sb[:, m, :], in1=bo_bank[:], op=ALU.add)
             x_plus_bo.append(sum_row)
+        spread_bias("b1", b1_all, range(0, 2))
         h_flipped = [flip_tokens(h_sb[:, m, :]) for m in range(TOKEN_TILES)]
         h_grouped = [group_tokens(h_flipped[m]) for m in range(TOKEN_TILES)]
+        spread_bias("b1", b1_all, range(2, 4))
         ln2_g_bank = spread(first_row["ln2_g"], "odd")
         ln2_b_bank = spread(first_row["ln2_b"], "odd")
         fln_g_bank = spread(first_row["fln_g"], "odd")
@@ -380,13 +390,13 @@ def tile_transformerblock_pa_kernel(
             )
             h2_flipped.append(flip_tokens(h2[:]))
         h2_grouped = [group_tokens(h2_flipped[m]) for m in range(TOKEN_TILES)]
+        spread_bias("b2", b2_all, range(4))
         regroup("vector", 1, "A", 0, 128)
         regroup("vector", 2, "A", 0, VECTOR_COLS[2])
         quantise(1, "A")
         h2_q = [quantise_tokens("h2_%d" % m, h2_grouped[m]) for m in range(TOKEN_TILES)]
         load_next()
         load_next()
-        nc.sync.dma_start(out=b2_all[:], in_=b2.partition_broadcast(P))
 
         for c in range(1, last + 2):
             if 3 < c + 1 <= last:

@@ -83,7 +83,7 @@ def tile_transformerblock_pa_kernel(
                     raw[(c, g)] = rows_of_pass[:, :, chunks[c][1] - first_col : chunks[c][1] - first_col + CHUNK]
             loaded.append((w, first_col, g))
 
-        def spread(first, tag):
+        def spread(vec_rows, first, tag):
             bank = psum.tile([P, 2 * BANK], BF16, tag=tag)
             for s in range(2):
                 row = first + s
@@ -96,9 +96,9 @@ def tile_transformerblock_pa_kernel(
                 )
             return bank
 
-        def spread_bias(key, bias, banks_of_bias):
+        def spread_bias(vec_rows, first, bias, banks_of_bias):
             for i in banks_of_bias:
-                bank = spread(first_row[key] + 2 * i, "odd")
+                bank = spread(vec_rows, first + 2 * i, "odd")
                 nc.scalar.copy(out=bias[:, i * 2 * BANK : (i + 1) * 2 * BANK], in_=bank[:])
 
         def flip_tokens(token_rows):
@@ -245,6 +245,8 @@ def tile_transformerblock_pa_kernel(
 
         vec_rows = consts.tile([P, BANK], BF16)
         nc.vector.memset(vec_rows[:], 0.0)
+        b2_rows = consts.tile([P, BANK], BF16)
+        nc.vector.memset(b2_rows[:], 0.0)
         first_row = {}
         filled = []
 
@@ -281,24 +283,24 @@ def tile_transformerblock_pa_kernel(
                 out=wo_rows[:, g, :, :], in_=Wo[g * K_PASS : (g + 1) * K_PASS, :].rearrange("(p t) n -> p t n", p=P)
             )
             raw[(0, g)] = wo_rows[:, g, :, :]
-        load_vector(nc.sync, "b2", b2)
+        nc.sync.dma_start(out=b2_rows[0 : F // BANK, :], in_=b2.rearrange("(r c) -> r c", c=BANK))
         for i in range(RAW_BUFS - 1):
             load_next()
 
-        bo_bank = spread(first_row["bo"], "even")
+        bo_bank = spread(vec_rows, first_row["bo"], "even")
         x_plus_bo = []
         for m in range(TOKEN_TILES):
             sum_row = rows.tile([P, D], F32, tag="row")
             nc.vector.tensor_tensor(out=sum_row[:], in0=x_sb[:, m, :], in1=bo_bank[:], op=ALU.add)
             x_plus_bo.append(sum_row)
-        spread_bias("b1", b1_all, range(0, 2))
+        spread_bias(vec_rows, first_row["b1"], b1_all, range(0, 2))
         h_flipped = [flip_tokens(h_sb[:, m, :]) for m in range(TOKEN_TILES)]
         h_grouped = [group_tokens(h_flipped[m]) for m in range(TOKEN_TILES)]
-        spread_bias("b1", b1_all, range(2, 4))
-        ln2_g_bank = spread(first_row["ln2_g"], "odd")
-        ln2_b_bank = spread(first_row["ln2_b"], "odd")
-        fln_g_bank = spread(first_row["fln_g"], "odd")
-        fln_b_bank = spread(first_row["fln_b"], "odd")
+        spread_bias(vec_rows, first_row["b1"], b1_all, range(2, 4))
+        ln2_g_bank = spread(vec_rows, first_row["ln2_g"], "odd")
+        ln2_b_bank = spread(vec_rows, first_row["ln2_b"], "odd")
+        fln_g_bank = spread(vec_rows, first_row["fln_g"], "odd")
+        fln_b_bank = spread(vec_rows, first_row["fln_b"], "odd")
 
         regroup("vector", 0, "A", 0, 672)
         regroup("scalar", 0, "A", 672, CHUNK)
@@ -390,7 +392,7 @@ def tile_transformerblock_pa_kernel(
             )
             h2_flipped.append(flip_tokens(h2[:]))
         h2_grouped = [group_tokens(h2_flipped[m]) for m in range(TOKEN_TILES)]
-        spread_bias("b2", b2_all, range(4))
+        spread_bias(b2_rows, 0, b2_all, range(4))
         regroup("vector", 1, "A", 0, 128)
         regroup("vector", 2, "A", 0, VECTOR_COLS[2])
         quantise(1, "A")

@@ -21,13 +21,15 @@ F = 4096
 PASSES = D // K_PASS
 BANK = 512
 CHUNK = 1024
-LOAD_COLS = 2048
+SINGLE_CHUNKS = 3
 RAW_BUFS = 6
 ROW_BUFS = 8
 RUN = 4
 EPS = 1e-5
-VECTOR_COLS = [0, 0, 256, 256, 256, 256, 256, 256, 256]
-POOL_COLS = [0, 512, 480, 480, 480, 480, 480, 480, 480]
+VECTOR_COLS = [0, 0, 256, 320, 320, 320, 320, 320, 320]
+HEAD_A = 704
+HEAD_B = 704
+POOL_COLS = [0, 512, 448, 448, 448, 448, 448, 448, 448]
 
 FLOPS = 2 * TOKENS * D * (D + 2 * F)
 
@@ -43,11 +45,9 @@ def tile_transformerblock_pa_kernel(
         for first_col in range(0, F, CHUNK):
             chunks.append((w, first_col))
     last = len(chunks) - 1
-    loads = []
-    for w in (W1, W2):
-        for first_col in range(0, F, LOAD_COLS):
-            for g in range(PASSES):
-                loads.append((w, first_col, g))
+    units = [(c, None) for c in range(SINGLE_CHUNKS)]
+    for c in range(SINGLE_CHUNKS, last + 1, 2):
+        units += [(c, g) for g in range(PASSES)]
     pieces = {"A": (0, 0, CHUNK), "B": (1, 0, CHUNK)}
 
     with ExitStack() as ctx:
@@ -68,25 +68,37 @@ def tile_transformerblock_pa_kernel(
         loaded = []
 
         def load_next():
-            if len(loaded) == len(loads):
+            if len(loaded) == len(units):
                 return
-            w, first_col, g = loads[len(loaded)]
-            rows_of_pass = raw_pool.tile([P, PACK, LOAD_COLS], BF16, tag="raw")
-            nc.sync.dma_start(
-                out=rows_of_pass[:],
-                in_=w[g * K_PASS : (g + 1) * K_PASS, first_col : first_col + LOAD_COLS].rearrange(
-                    "(p t) n -> p t n", p=P
-                ),
-            )
-            for c in range(1, last + 1):
-                if chunks[c][0] is w and first_col <= chunks[c][1] < first_col + LOAD_COLS:
-                    raw[(c, g)] = rows_of_pass[:, :, chunks[c][1] - first_col : chunks[c][1] - first_col + CHUNK]
-            loaded.append((w, first_col, g))
+            c, g = units[len(loaded)]
+            w, first_col = chunks[c]
+            if g is None:
+                rows_of_chunk = raw_pool.tile([P, PASSES, PACK, CHUNK], BF16, tag="raw")
+                for g in range(PASSES):
+                    nc.sync.dma_start(
+                        out=rows_of_chunk[:, g, :, :],
+                        in_=w[g * K_PASS : (g + 1) * K_PASS, first_col : first_col + CHUNK].rearrange(
+                            "(p t) n -> p t n", p=P
+                        ),
+                    )
+                    raw[(c, g)] = rows_of_chunk[:, g, :, :]
+            else:
+                rows_of_pass = raw_pool.tile([P, PACK, 2 * CHUNK], BF16, tag="raw")
+                nc.sync.dma_start(
+                    out=rows_of_pass[:],
+                    in_=w[g * K_PASS : (g + 1) * K_PASS, first_col : first_col + 2 * CHUNK].rearrange(
+                        "(p t) n -> p t n", p=P
+                    ),
+                )
+                for i in range(2):
+                    raw[(c + i, g)] = rows_of_pass[:, :, i * CHUNK : (i + 1) * CHUNK]
+            loaded.append(c)
 
-        def spread(vec_rows, first, tag):
+        def spread(key, i, tag):
+            vec_rows, first = first_row[key]
             bank = psum.tile([P, 2 * BANK], BF16, tag=tag)
             for s in range(2):
-                row = first + s
+                row = first + 2 * i + s
                 nc.tensor.matmul(
                     out=bank[:, s * BANK : (s + 1) * BANK],
                     lhsT=ident[:, row : row + 1].to_broadcast([P, P]),
@@ -96,10 +108,12 @@ def tile_transformerblock_pa_kernel(
                 )
             return bank
 
-        def spread_bias(vec_rows, first, bias, banks_of_bias):
-            for i in banks_of_bias:
-                bank = spread(vec_rows, first + 2 * i, "odd")
-                nc.scalar.copy(out=bias[:, i * 2 * BANK : (i + 1) * 2 * BANK], in_=bank[:])
+        def keep_bias(engine, bias, i, bank):
+            dst = bias[:, i * 2 * BANK : (i + 1) * 2 * BANK]
+            if engine == "vector":
+                nc.vector.tensor_copy(out=dst, in_=bank[:])
+            else:
+                nc.scalar.copy(out=dst, in_=bank[:])
 
         def flip_tokens(token_rows):
             words = token_rows.bitcast(F32)
@@ -243,26 +257,27 @@ def tile_transformerblock_pa_kernel(
             elif n == CHUNK // BANK - 1:
                 nc.sync.dma_start(out=out_rows[:, first_col : first_col + CHUNK], in_=staged[(c, m)][:])
 
-        vec_rows = consts.tile([P, BANK], BF16)
-        nc.vector.memset(vec_rows[:], 0.0)
-        b2_rows = consts.tile([P, BANK], BF16)
-        nc.vector.memset(b2_rows[:], 0.0)
         first_row = {}
-        filled = []
 
-        def load_vector(queue, key, vec):
-            row = len(filled)
-            n_rows = vec.shape[0] // BANK
-            queue.dma_start(out=vec_rows[row : row + n_rows, :], in_=vec.rearrange("(r c) -> r c", c=BANK))
-            first_row[key] = row
-            filled.extend(range(row, row + n_rows))
+        def load_vectors(queue, vectors):
+            vec_rows = consts.tile([P, BANK], BF16, name="rows_" + vectors[0][0])
+            nc.vector.memset(vec_rows[:], 0.0)
+            row = 0
+            for key, vec in vectors:
+                n_rows = vec.shape[0] // BANK
+                queue.dma_start(out=vec_rows[row : row + n_rows, :], in_=vec.rearrange("(r c) -> r c", c=BANK))
+                first_row[key] = (vec_rows, row)
+                row += n_rows
 
-        load_vector(nc.scalar, "bo", bo)
-        load_vector(nc.scalar, "b1", b1)
+        load_vectors(nc.scalar, [("b1", b1), ("b2", b2), ("bo", bo)])
+        load_next()
+        h_sb = rows.tile([P, TOKEN_TILES, D], BF16, tag="row")
+        nc.sync.dma_start(
+            out=h_sb[:], in_=h_attn.flatten_outer_dims().rearrange("(m p) d -> p m d", p=P)
+        )
         x_sb = rows.tile([P, TOKEN_TILES, D], BF16, tag="row")
         nc.sync.dma_start(out=x_sb[:], in_=x.flatten_outer_dims().rearrange("(m p) d -> p m d", p=P))
-        for key, vec in (("ln2_g", ln2_g), ("ln2_b", ln2_b), ("fln_g", fln_g), ("fln_b", fln_b)):
-            load_vector(nc.sync, key, vec)
+        load_vectors(nc.sync, [("ln2_g", ln2_g), ("ln2_b", ln2_b), ("fln_g", fln_g), ("fln_b", fln_b)])
         ident = consts.tile([P, P], BF16)
         make_identity(nc, ident[:])
         ident_words = consts.tile([P, P], F32)
@@ -271,90 +286,97 @@ def tile_transformerblock_pa_kernel(
         nc.gpsimd.memset(eps_column[:], EPS)
         warm = consts.tile([P, 1], F32)
         nc.scalar.activation(out=warm[:], in_=eps_column[:], func=ACT.Abs_reciprocal_sqrt)
-        h_sb = rows.tile([P, TOKEN_TILES, D], BF16, tag="row")
-        nc.sync.dma_start(
-            out=h_sb[:], in_=h_attn.flatten_outer_dims().rearrange("(m p) d -> p m d", p=P)
-        )
         b1_all = consts.tile([P, F], BF16)
         b2_all = consts.tile([P, F], BF16)
-        wo_rows = raw_pool.tile([P, PASSES, PACK, CHUNK], BF16, tag="raw")
-        for g in range(PASSES):
-            nc.sync.dma_start(
-                out=wo_rows[:, g, :, :], in_=Wo[g * K_PASS : (g + 1) * K_PASS, :].rearrange("(p t) n -> p t n", p=P)
-            )
-            raw[(0, g)] = wo_rows[:, g, :, :]
-        nc.sync.dma_start(out=b2_rows[0 : F // BANK, :], in_=b2.rearrange("(r c) -> r c", c=BANK))
         for i in range(RAW_BUFS - 1):
             load_next()
 
-        bo_bank = spread(vec_rows, first_row["bo"], "even")
+        b1_banks = [spread("b1", i, "odd") for i in range(4)]
+        keep_bias("scalar", b1_all, 0, b1_banks[0])
+        regroup("scalar", 0, "A", HEAD_A, CHUNK)
+        regroup("vector", 0, "A", 0, HEAD_A)
+        keep_bias("scalar", b1_all, 1, b1_banks[1])
+        keep_bias("scalar", b1_all, 2, b1_banks[2])
+        bo_bank = spread("bo", 0, "odd")
+        b2_banks = [spread("b2", i, "odd") for i in range(2)]
+        quantise(0, "A")
+        regroup("scalar", 0, "B", HEAD_B, CHUNK)
+        regroup("vector", 0, "B", 0, HEAD_B)
+        h_flipped = [flip_tokens(h_sb[:, m, :]) for m in range(TOKEN_TILES)]
+        h_grouped = [group_tokens(h_flipped[m]) for m in range(TOKEN_TILES)]
+        quantise(0, "B")
+        h_q = [quantise_tokens("h%d" % m, h_grouped[m]) for m in range(TOKEN_TILES)]
+        keep_bias("scalar", b1_all, 3, b1_banks[3])
+        b2_banks.append(spread("b2", 2, "odd"))
+        keep_bias("scalar", b2_all, 0, b2_banks[0])
+        keep_bias("scalar", b2_all, 1, b2_banks[1])
+        regroup("scalar", 1, "A", 128, BANK)
+        keep_bias("scalar", b2_all, 2, b2_banks[2])
         x_plus_bo = []
         for m in range(TOKEN_TILES):
+            multiply(0, "A", m, h_q)
+            multiply(0, "B", m, h_q)
             sum_row = rows.tile([P, D], F32, tag="row")
             nc.vector.tensor_tensor(out=sum_row[:], in0=x_sb[:, m, :], in1=bo_bank[:], op=ALU.add)
             x_plus_bo.append(sum_row)
-        spread_bias(vec_rows, first_row["b1"], b1_all, range(0, 2))
-        h_flipped = [flip_tokens(h_sb[:, m, :]) for m in range(TOKEN_TILES)]
-        h_grouped = [group_tokens(h_flipped[m]) for m in range(TOKEN_TILES)]
-        spread_bias(vec_rows, first_row["b1"], b1_all, range(2, 4))
-        ln2_g_bank = spread(vec_rows, first_row["ln2_g"], "odd")
-        ln2_b_bank = spread(vec_rows, first_row["ln2_b"], "odd")
-        fln_g_bank = spread(vec_rows, first_row["fln_g"], "odd")
-        fln_b_bank = spread(vec_rows, first_row["fln_b"], "odd")
-
-        regroup("vector", 0, "A", 0, 672)
-        regroup("scalar", 0, "A", 672, CHUNK)
-        h_q = [quantise_tokens("h%d" % m, h_grouped[m]) for m in range(TOKEN_TILES)]
-        quantise(0, "A")
-        multiply(0, "A", 0, h_q)
-        regroup("scalar", 0, "B", 432, CHUNK)
-        regroup("vector", 0, "B", 0, 432)
-        quantise(0, "B")
-        multiply(0, "B", 0, h_q)
-        multiply(0, "A", 1, h_q)
-        multiply(0, "B", 1, h_q)
+        keep_bias("scalar", b2_all, 3, spread("b2", 3, "odd"))
+        ln2_g_bank = spread("ln2_g", 0, "odd")
+        ln2_b_bank = spread("ln2_b", 0, "odd")
+        fln_g_bank = spread("fln_g", 0, "odd")
+        fln_b_bank = spread("fln_b", 0, "odd")
         load_next()
 
         regroup("pool", 1, "A", BANK, CHUNK)
-        regroup("pool", 2, "A", BANK, CHUNK)
         regroup("pool", 1, "B", BANK, CHUNK)
+        regroup("pool", 2, "A", BANK, CHUNK)
         regroup("pool", 2, "B", CHUNK - POOL_COLS[2], CHUNK)
         regroup("pool", 2, "B", 224, CHUNK - POOL_COLS[2])
-        regroup("scalar", 1, "A", 128, BANK)
         half_sums = small.tile([P, TOKEN_TILES, 2], F32, tag="half_sums")
         scaled_halves = small.tile([P, TOKEN_TILES, 2], F32, tag="scaled_halves")
         minus_mean = small.tile([P, TOKEN_TILES, 1], F32, tag="minus_mean")
         sum_sq = small.tile([P, TOKEN_TILES, 1], F32, tag="sum_sq")
         rstd = small.tile([P, TOKEN_TILES, 1], F32, tag="rstd")
-        r = []
-        for m in range(TOKEN_TILES):
-            r_row = rows.tile([P, D], F32, tag="row")
-            for n in range(D // BANK):
-                cols = slice(n * BANK, (n + 1) * BANK)
-                nc.vector.scalar_tensor_tensor(
-                    out=r_row[:, cols],
-                    in0=banks[(0, m, n)][:],
-                    scalar=1.0,
-                    in1=x_plus_bo[m][:, cols],
-                    op0=ALU.mult,
-                    op1=ALU.add,
-                    accum_out=half_sums[:, m, n : n + 1],
-                )
+        y = [rows.tile([P, D], F32, tag="row", name="y%d" % m) for m in range(TOKEN_TILES)]
+        r = y
+        scaled = x_plus_bo
+
+        def add_residual(m, n):
+            cols = slice(n * BANK, (n + 1) * BANK)
+            nc.vector.scalar_tensor_tensor(
+                out=y[m][:, cols],
+                in0=banks[(0, m, n)][:],
+                scalar=1.0,
+                in1=x_plus_bo[m][:, cols],
+                op0=ALU.mult,
+                op1=ALU.add,
+                accum_out=half_sums[:, m, n : n + 1],
+            )
+
+        def centre_and_scale(m):
+            nc.vector.scalar_tensor_tensor(
+                out=scaled[m][:], in0=y[m][:], scalar=minus_mean[:, m, :], in1=ln2_g_bank[:], op0=ALU.add, op1=ALU.mult
+            )
+
+        def mean_of(m, sums, parts, minus_mean):
             nc.scalar.activation(
-                out=scaled_halves[:, m, :],
-                in_=half_sums[:, m, :],
+                out=scaled_halves[:, m, 0:parts],
+                in_=sums,
                 func=ACT.Copy,
                 scale=-1.0 / D,
                 accum_out=minus_mean[:, m, :],
             )
-            square_sum(m, r_row, minus_mean, sum_sq)
-            rstd_of(m, sum_sq, rstd)
-            r.append(r_row)
+
         for m in range(TOKEN_TILES):
-            nc.vector.scalar_tensor_tensor(
-                out=r[m][:], in0=r[m][:], scalar=minus_mean[:, m, :], in1=ln2_g_bank[:], op0=ALU.add, op1=ALU.mult
-            )
-        regroup("scalar", 1, "B", 0, BANK)
+            for n in range(D // BANK):
+                add_residual(m, n)
+        mean_of(0, half_sums[:, 0, :], 2, minus_mean)
+        square_sum(0, y[0], minus_mean, sum_sq)
+        mean_of(1, half_sums[:, 1, :], 2, minus_mean)
+        rstd_of(0, sum_sq, rstd)
+        square_sum(1, y[1], minus_mean, sum_sq)
+        rstd_of(1, sum_sq, rstd)
+        for m in range(TOKEN_TILES):
+            centre_and_scale(m)
         row_sums = small.tile([P, TOKEN_TILES, 1], F32, tag="row_sums")
         minus_mean_2 = small.tile([P, TOKEN_TILES, 1], F32, tag="minus_mean")
         sum_sq_2 = small.tile([P, TOKEN_TILES, 1], F32, tag="sum_sq")
@@ -362,7 +384,7 @@ def tile_transformerblock_pa_kernel(
         for m in range(TOKEN_TILES):
             nc.vector.scalar_tensor_tensor(
                 out=r[m][:],
-                in0=r[m][:],
+                in0=scaled[m][:],
                 scalar=rstd[:, m, :],
                 in1=ln2_b_bank[:],
                 op0=ALU.mult,
@@ -370,11 +392,13 @@ def tile_transformerblock_pa_kernel(
                 accum_out=row_sums[:, m, :],
             )
             nc.sync.dma_start(out=r_out[m * P : (m + 1) * P, :], in_=r[m][:])
-            nc.scalar.activation(
-                out=minus_mean_2[:, m, :], in_=row_sums[:, m, :], func=ACT.Copy, scale=-1.0 / D
-            )
-            square_sum(m, r[m], minus_mean_2, sum_sq_2)
-            rstd_of(m, sum_sq_2, rstd_2)
+        mean_of(0, row_sums[:, 0, :], 1, minus_mean_2)
+        square_sum(0, r[0], minus_mean_2, sum_sq_2)
+        mean_of(1, row_sums[:, 1, :], 1, minus_mean_2)
+        rstd_of(0, sum_sq_2, rstd_2)
+        square_sum(1, r[1], minus_mean_2, sum_sq_2)
+        rstd_of(1, sum_sq_2, rstd_2)
+        regroup("scalar", 1, "B", 0, BANK)
         centred = []
         for m in range(TOKEN_TILES):
             centred_row = rows.tile([P, D], F32, tag="row")
@@ -382,8 +406,6 @@ def tile_transformerblock_pa_kernel(
                 out=centred_row[:], in0=r[m][:], scalar=minus_mean_2[:, m, :], in1=fln_g_bank[:], op0=ALU.add, op1=ALU.mult
             )
             centred.append(centred_row)
-        regroup("scalar", 2, "A", VECTOR_COLS[2], BANK)
-        regroup("scalar", 2, "B", 0, 224)
         h2_flipped = []
         for m in range(TOKEN_TILES):
             h2 = acts.tile([P, D], BF16, tag="h2")
@@ -391,8 +413,10 @@ def tile_transformerblock_pa_kernel(
                 out=h2[:], in0=centred[m][:], scalar=rstd_2[:, m, :], in1=fln_b_bank[:], op0=ALU.mult, op1=ALU.add
             )
             h2_flipped.append(flip_tokens(h2[:]))
-        h2_grouped = [group_tokens(h2_flipped[m]) for m in range(TOKEN_TILES)]
-        spread_bias(b2_rows, 0, b2_all, range(4))
+        h2_grouped = [group_tokens(h2_flipped[0])]
+        regroup("scalar", 2, "B", 0, 224)
+        h2_grouped.append(group_tokens(h2_flipped[1]))
+        regroup("scalar", 2, "A", VECTOR_COLS[2], BANK)
         regroup("vector", 1, "A", 0, 128)
         regroup("vector", 2, "A", 0, VECTOR_COLS[2])
         quantise(1, "A")
@@ -407,8 +431,10 @@ def tile_transformerblock_pa_kernel(
                 quantise_and_multiply(c, h2_q)
             if c == 1:
                 regroup("vector", 3, "A", 0, VECTOR_COLS[3])
+            if 2 < c + 1 <= last:
+                regroup("pool", c + 1, "B", CHUNK - POOL_COLS[c + 1] // 2, CHUNK)
             if c + 2 <= last:
-                regroup("pool", c + 2, "B", CHUNK - POOL_COLS[c + 2], CHUNK)
+                regroup("pool", c + 2, "B", CHUNK - POOL_COLS[c + 2], CHUNK - POOL_COLS[c + 2] // 2)
             if c + 1 <= last:
                 regroup("scalar", c + 1, "A", CHUNK if c + 1 == 2 else VECTOR_COLS[c + 1], CHUNK)
                 if c + 1 > 2:

@@ -29,7 +29,7 @@ EPS = 1e-5
 VECTOR_COLS = [0, 0, 256, 320, 320, 320, 320, 320, 320]
 HEAD_A = 704
 HEAD_B = 704
-POOL_COLS = [0, 512, 448, 448, 448, 448, 448, 448, 448]
+POOL_COLS = [0, 512, 480, 480, 480, 480, 480, 480, 480]
 
 FLOPS = 2 * TOKENS * D * (D + 2 * F)
 
@@ -67,7 +67,7 @@ def tile_transformerblock_pa_kernel(
         banks = {}
         loaded = []
 
-        def load_next():
+        def load_next(between=None):
             if len(loaded) == len(units):
                 return
             c, g = units[len(loaded)]
@@ -82,6 +82,8 @@ def tile_transformerblock_pa_kernel(
                         ),
                     )
                     raw[(c, g)] = rows_of_chunk[:, g, :, :]
+                    if between and g == 0:
+                        between()
             else:
                 rows_of_pass = raw_pool.tile([P, PACK, 2 * CHUNK], BF16, tag="raw")
                 nc.sync.dma_start(
@@ -210,6 +212,8 @@ def tile_transformerblock_pa_kernel(
             if c > 1:
                 quantise(c, "A")
             multiply(c, "A", 0, tokens_q)
+            if c == last:
+                empty_bank(c - 1, 1, 0)
             quantise(c, "B")
             multiply(c, "B", 0, tokens_q)
             multiply(c, "A", 1, tokens_q)
@@ -258,32 +262,35 @@ def tile_transformerblock_pa_kernel(
                 nc.sync.dma_start(out=out_rows[:, first_col : first_col + CHUNK], in_=staged[(c, m)][:])
 
         first_row = {}
+        rows_of_biases = consts.tile([P, BANK], BF16)
+        rows_of_norms = consts.tile([P, BANK], BF16)
+        nc.gpsimd.memset(rows_of_biases[:].bitcast(U32), 0)
+        eps_column = consts.tile([P, 1], F32)
+        nc.gpsimd.memset(eps_column[:], EPS)
+        ident = consts.tile([P, P], BF16)
+        make_identity(nc, ident[:])
+        nc.gpsimd.memset(rows_of_norms[:].bitcast(U32), 0)
+        ident_words = consts.tile([P, P], F32)
+        make_identity(nc, ident_words[:])
 
-        def load_vectors(queue, vectors):
-            vec_rows = consts.tile([P, BANK], BF16, name="rows_" + vectors[0][0])
-            nc.vector.memset(vec_rows[:], 0.0)
+        def load_vectors(vec_rows, vectors):
             row = 0
             for key, vec in vectors:
                 n_rows = vec.shape[0] // BANK
-                queue.dma_start(out=vec_rows[row : row + n_rows, :], in_=vec.rearrange("(r c) -> r c", c=BANK))
+                nc.sync.dma_start(out=vec_rows[row : row + n_rows, :], in_=vec.rearrange("(r c) -> r c", c=BANK))
                 first_row[key] = (vec_rows, row)
                 row += n_rows
 
-        load_vectors(nc.scalar, [("b1", b1), ("b2", b2), ("bo", bo)])
-        load_next()
-        h_sb = rows.tile([P, TOKEN_TILES, D], BF16, tag="row")
-        nc.sync.dma_start(
-            out=h_sb[:], in_=h_attn.flatten_outer_dims().rearrange("(m p) d -> p m d", p=P)
-        )
         x_sb = rows.tile([P, TOKEN_TILES, D], BF16, tag="row")
         nc.sync.dma_start(out=x_sb[:], in_=x.flatten_outer_dims().rearrange("(m p) d -> p m d", p=P))
-        load_vectors(nc.sync, [("ln2_g", ln2_g), ("ln2_b", ln2_b), ("fln_g", fln_g), ("fln_b", fln_b)])
-        ident = consts.tile([P, P], BF16)
-        make_identity(nc, ident[:])
-        ident_words = consts.tile([P, P], F32)
-        make_identity(nc, ident_words[:])
-        eps_column = consts.tile([P, 1], F32)
-        nc.gpsimd.memset(eps_column[:], EPS)
+        load_vectors(rows_of_biases, [("bo", bo), ("b1", b1), ("b2", b2)])
+        h_sb = rows.tile([P, TOKEN_TILES, D], BF16, tag="row")
+        load_next(
+            between=lambda: nc.sync.dma_start(
+                out=h_sb[:], in_=h_attn.flatten_outer_dims().rearrange("(m p) d -> p m d", p=P)
+            )
+        )
+        load_vectors(rows_of_norms, [("ln2_g", ln2_g), ("ln2_b", ln2_b), ("fln_g", fln_g), ("fln_b", fln_b)])
         warm = consts.tile([P, 1], F32)
         nc.scalar.activation(out=warm[:], in_=eps_column[:], func=ACT.Abs_reciprocal_sqrt)
         b1_all = consts.tile([P, F], BF16)
@@ -291,39 +298,40 @@ def tile_transformerblock_pa_kernel(
         for i in range(RAW_BUFS - 1):
             load_next()
 
+        bo_bank = spread("bo", 0, "even")
+        x_plus_bo = [rows.tile([P, D], F32, tag="row", name="x_plus_bo%d" % m) for m in range(TOKEN_TILES)]
+        for n in range(D // BANK):
+            cols = slice(n * BANK, (n + 1) * BANK)
+            for m in range(TOKEN_TILES):
+                nc.vector.tensor_tensor(
+                    out=x_plus_bo[m][:, cols], in0=x_sb[:, m, cols], in1=bo_bank[:, cols], op=ALU.add
+                )
         b1_banks = [spread("b1", i, "odd") for i in range(4)]
         keep_bias("scalar", b1_all, 0, b1_banks[0])
         regroup("scalar", 0, "A", HEAD_A, CHUNK)
         regroup("vector", 0, "A", 0, HEAD_A)
-        keep_bias("scalar", b1_all, 1, b1_banks[1])
-        keep_bias("scalar", b1_all, 2, b1_banks[2])
-        bo_bank = spread("bo", 0, "odd")
-        b2_banks = [spread("b2", i, "odd") for i in range(2)]
-        quantise(0, "A")
-        regroup("scalar", 0, "B", HEAD_B, CHUNK)
-        regroup("vector", 0, "B", 0, HEAD_B)
+        b2_banks = [spread("b2", 0, "odd")]
         h_flipped = [flip_tokens(h_sb[:, m, :]) for m in range(TOKEN_TILES)]
         h_grouped = [group_tokens(h_flipped[m]) for m in range(TOKEN_TILES)]
-        quantise(0, "B")
+        quantise(0, "A")
         h_q = [quantise_tokens("h%d" % m, h_grouped[m]) for m in range(TOKEN_TILES)]
+        multiply(0, "A", 0, h_q)
+        multiply(0, "A", 1, h_q)
+        keep_bias("scalar", b1_all, 1, b1_banks[1])
+        b2_banks.append(spread("b2", 1, "odd"))
+        regroup("scalar", 0, "B", HEAD_B, CHUNK)
+        regroup("vector", 0, "B", 0, HEAD_B)
+        quantise(0, "B")
+        multiply(0, "B", 0, h_q)
+        multiply(0, "B", 1, h_q)
+        keep_bias("scalar", b1_all, 2, b1_banks[2])
         keep_bias("scalar", b1_all, 3, b1_banks[3])
-        b2_banks.append(spread("b2", 2, "odd"))
+        b2_banks += [spread("b2", i, "odd") for i in (2, 3)]
         keep_bias("scalar", b2_all, 0, b2_banks[0])
         keep_bias("scalar", b2_all, 1, b2_banks[1])
-        regroup("scalar", 1, "A", 128, BANK)
-        keep_bias("scalar", b2_all, 2, b2_banks[2])
-        x_plus_bo = []
-        for m in range(TOKEN_TILES):
-            multiply(0, "A", m, h_q)
-            multiply(0, "B", m, h_q)
-            sum_row = rows.tile([P, D], F32, tag="row")
-            nc.vector.tensor_tensor(out=sum_row[:], in0=x_sb[:, m, :], in1=bo_bank[:], op=ALU.add)
-            x_plus_bo.append(sum_row)
-        keep_bias("scalar", b2_all, 3, spread("b2", 3, "odd"))
         ln2_g_bank = spread("ln2_g", 0, "odd")
         ln2_b_bank = spread("ln2_b", 0, "odd")
-        fln_g_bank = spread("fln_g", 0, "odd")
-        fln_b_bank = spread("fln_b", 0, "odd")
+        regroup("scalar", 1, "A", 128, BANK)
         load_next()
 
         regroup("pool", 1, "A", BANK, CHUNK)
@@ -377,6 +385,10 @@ def tile_transformerblock_pa_kernel(
         rstd_of(1, sum_sq, rstd)
         for m in range(TOKEN_TILES):
             centre_and_scale(m)
+        keep_bias("scalar", b2_all, 2, b2_banks[2])
+        keep_bias("scalar", b2_all, 3, b2_banks[3])
+        fln_g_bank = spread("fln_g", 0, "odd")
+        fln_b_bank = spread("fln_b", 0, "odd")
         row_sums = small.tile([P, TOKEN_TILES, 1], F32, tag="row_sums")
         minus_mean_2 = small.tile([P, TOKEN_TILES, 1], F32, tag="minus_mean")
         sum_sq_2 = small.tile([P, TOKEN_TILES, 1], F32, tag="sum_sq")
@@ -442,4 +454,5 @@ def tile_transformerblock_pa_kernel(
             for cc, m in ((c - 1, 1), (c, 0)):
                 if 1 <= cc <= last:
                     for n in range(CHUNK // BANK):
-                        empty_bank(cc, m, n)
+                        if (cc, m, n) != (last - 1, 1, 0):
+                            empty_bank(cc, m, n)

@@ -23,7 +23,7 @@ BANK = 512
 CHUNK = 1024
 SINGLE_CHUNKS = 3
 RAW_BUFS = 6
-ROW_BUFS = 8
+ROW_BUFS = 12
 RUN = 4
 EPS = 1e-5
 VECTOR_COLS = [0, 0, 256, 320, 320, 320, 320, 320, 320]
@@ -38,7 +38,7 @@ def tile_transformerblock_pa_kernel(
     tc, h_attn, x, Wo, bo, ln2_g, ln2_b, fln_g, fln_b, W1, b1, W2, b2, out_0, out_1, out_2
 ):
     nc = tc.nc
-    r_out = out_0.flatten_outer_dims()
+    r_out = out_0.flatten_outer_dims().rearrange("(p m) d -> m p d", p=P)
 
     chunks = [(Wo, 0)]
     for w in (W1, W2):
@@ -57,7 +57,7 @@ def tile_transformerblock_pa_kernel(
         acts = ctx.enter_context(tc.tile_pool(name="acts", bufs=2))
         raw_pool = ctx.enter_context(tc.tile_pool(name="raw", bufs=RAW_BUFS))
         grouped_pool = ctx.enter_context(tc.tile_pool(name="grouped", bufs=2))
-        quantised = ctx.enter_context(tc.tile_pool(name="quantised", bufs=3))
+        quantised = ctx.enter_context(tc.tile_pool(name="quantised", bufs=2))
         psum = ctx.enter_context(tc.psum_pool(name="psum", bufs=4))
         ctx.enter_context(tc.manual_schedule())
 
@@ -252,7 +252,7 @@ def tile_transformerblock_pa_kernel(
                 in1=bias[:, first_col + n * BANK : first_col + (n + 1) * BANK],
                 op=ALU.add,
             )
-            out_rows = out.flatten_outer_dims()[m * P : (m + 1) * P, :]
+            out_rows = out.flatten_outer_dims().rearrange("(p m) f -> m p f", p=P)[m, :, :]
             if c == last:
                 nc.sync.dma_start(
                     out=out_rows[:, first_col + n * BANK : first_col + (n + 1) * BANK],
@@ -282,12 +282,12 @@ def tile_transformerblock_pa_kernel(
                 row += n_rows
 
         x_sb = rows.tile([P, TOKEN_TILES, D], BF16, tag="row")
-        nc.sync.dma_start(out=x_sb[:], in_=x.flatten_outer_dims().rearrange("(m p) d -> p m d", p=P))
+        nc.sync.dma_start(out=x_sb[:], in_=x.flatten_outer_dims().rearrange("(p m) d -> p m d", p=P))
         load_vectors(rows_of_biases, [("bo", bo), ("b1", b1), ("b2", b2)])
         h_sb = rows.tile([P, TOKEN_TILES, D], BF16, tag="row")
         load_next(
             between=lambda: nc.sync.dma_start(
-                out=h_sb[:], in_=h_attn.flatten_outer_dims().rearrange("(m p) d -> p m d", p=P)
+                out=h_sb[:], in_=h_attn.flatten_outer_dims().rearrange("(p m) d -> p m d", p=P)
             )
         )
         load_vectors(rows_of_norms, [("ln2_g", ln2_g), ("ln2_b", ln2_b), ("fln_g", fln_g), ("fln_b", fln_b)])
@@ -403,7 +403,7 @@ def tile_transformerblock_pa_kernel(
                 op1=ALU.add,
                 accum_out=row_sums[:, m, :],
             )
-            nc.sync.dma_start(out=r_out[m * P : (m + 1) * P, :], in_=r[m][:])
+            nc.sync.dma_start(out=r_out[m, :, :], in_=r[m][:])
         mean_of(0, row_sums[:, 0, :], 1, minus_mean_2)
         square_sum(0, r[0], minus_mean_2, sum_sq_2)
         mean_of(1, row_sums[:, 1, :], 1, minus_mean_2)

@@ -26,7 +26,7 @@ RAW_BUFS = 6
 ROW_BUFS = 12
 RUN = 4
 EPS = 1e-5
-VECTOR_COLS = [0, 0, 256, 320, 320, 320, 320, 320, 320]
+VECTOR_COLS = [0, 0, 256, 192, 192, 192, 192, 192, 192]
 HEAD_A = 704
 HEAD_B = 704
 POOL_COLS = [0, 512, 480, 480, 480, 480, 480, 480, 480]

@@ -26,10 +26,10 @@ RAW_BUFS = 6
 ROW_BUFS = 12
 RUN = 4
 EPS = 1e-5
-VECTOR_COLS = [0, 0, 256, 192, 192, 192, 192, 192, 192]
+VECTOR_COLS = [0, 0, 0, 192, 192, 192, 192, 192, 192]
 HEAD_A = 704
 HEAD_B = 704
-POOL_COLS = [0, 512, 480, 480, 480, 480, 480, 480, 480]
+POOL_COLS = [0, 512, 512, 512, 512, 512, 512, 512, 512]
 
 FLOPS = 2 * TOKENS * D * (D + 2 * F)
 
@@ -262,14 +262,16 @@ def tile_transformerblock_pa_kernel(
                 nc.sync.dma_start(out=out_rows[:, first_col : first_col + CHUNK], in_=staged[(c, m)][:])
 
         first_row = {}
-        rows_of_biases = consts.tile([P, BANK], BF16)
+        rows_of_bo = consts.tile([P, BANK], BF16)
+        rows_of_b1 = consts.tile([P, BANK], BF16)
         rows_of_norms = consts.tile([P, BANK], BF16)
-        nc.gpsimd.memset(rows_of_biases[:].bitcast(U32), 0)
+        nc.gpsimd.memset(rows_of_bo[:].bitcast(U32), 0)
         eps_column = consts.tile([P, 1], F32)
         nc.gpsimd.memset(eps_column[:], EPS)
         ident = consts.tile([P, P], BF16)
         make_identity(nc, ident[:])
-        nc.gpsimd.memset(rows_of_norms[:].bitcast(U32), 0)
+        nc.vector.memset(rows_of_b1[:].bitcast(U32), 0)
+        nc.vector.memset(rows_of_norms[:].bitcast(U32), 0)
         ident_words = consts.tile([P, P], F32)
         make_identity(nc, ident_words[:])
 
@@ -281,9 +283,12 @@ def tile_transformerblock_pa_kernel(
                 first_row[key] = (vec_rows, row)
                 row += n_rows
 
-        x_sb = rows.tile([P, TOKEN_TILES, D], BF16, tag="row")
-        nc.sync.dma_start(out=x_sb[:], in_=x.flatten_outer_dims().rearrange("(p m) d -> p m d", p=P))
-        load_vectors(rows_of_biases, [("bo", bo), ("b1", b1), ("b2", b2)])
+        x_sb = rows.tile([P, D // BANK, TOKEN_TILES, BANK], BF16, tag="row")
+        x_view = x.flatten_outer_dims().rearrange("(p m) d -> p m d", p=P)
+        nc.sync.dma_start(out=x_sb[:, 0, :, :], in_=x_view[:, :, 0:BANK])
+        load_vectors(rows_of_bo, [("bo", bo)])
+        nc.sync.dma_start(out=x_sb[:, 1, :, :], in_=x_view[:, :, BANK:D])
+        load_vectors(rows_of_b1, [("b1", b1)])
         h_sb = rows.tile([P, TOKEN_TILES, D], BF16, tag="row")
         load_next(
             between=lambda: nc.sync.dma_start(
@@ -304,21 +309,21 @@ def tile_transformerblock_pa_kernel(
             cols = slice(n * BANK, (n + 1) * BANK)
             for m in range(TOKEN_TILES):
                 nc.vector.tensor_tensor(
-                    out=x_plus_bo[m][:, cols], in0=x_sb[:, m, cols], in1=bo_bank[:, cols], op=ALU.add
+                    out=x_plus_bo[m][:, cols], in0=x_sb[:, n, m, :], in1=bo_bank[:, cols], op=ALU.add
                 )
         b1_banks = [spread("b1", i, "odd") for i in range(4)]
         keep_bias("scalar", b1_all, 0, b1_banks[0])
         regroup("scalar", 0, "A", HEAD_A, CHUNK)
         regroup("vector", 0, "A", 0, HEAD_A)
-        b2_banks = [spread("b2", 0, "odd")]
         h_flipped = [flip_tokens(h_sb[:, m, :]) for m in range(TOKEN_TILES)]
         h_grouped = [group_tokens(h_flipped[m]) for m in range(TOKEN_TILES)]
         quantise(0, "A")
         h_q = [quantise_tokens("h%d" % m, h_grouped[m]) for m in range(TOKEN_TILES)]
         multiply(0, "A", 0, h_q)
         multiply(0, "A", 1, h_q)
+        ln2_g_bank = spread("ln2_g", 0, "odd")
         keep_bias("scalar", b1_all, 1, b1_banks[1])
-        b2_banks.append(spread("b2", 1, "odd"))
+        ln2_b_bank = spread("ln2_b", 0, "odd")
         regroup("scalar", 0, "B", HEAD_B, CHUNK)
         regroup("vector", 0, "B", 0, HEAD_B)
         quantise(0, "B")
@@ -326,12 +331,9 @@ def tile_transformerblock_pa_kernel(
         multiply(0, "B", 1, h_q)
         keep_bias("scalar", b1_all, 2, b1_banks[2])
         keep_bias("scalar", b1_all, 3, b1_banks[3])
-        b2_banks += [spread("b2", i, "odd") for i in (2, 3)]
-        keep_bias("scalar", b2_all, 0, b2_banks[0])
-        keep_bias("scalar", b2_all, 1, b2_banks[1])
-        ln2_g_bank = spread("ln2_g", 0, "odd")
-        ln2_b_bank = spread("ln2_b", 0, "odd")
-        regroup("scalar", 1, "A", 128, BANK)
+        fln_g_bank = spread("fln_g", 0, "odd")
+        fln_b_bank = spread("fln_b", 0, "odd")
+        regroup("scalar", 1, "A", 0, BANK)
         load_next()
 
         regroup("pool", 1, "A", BANK, CHUNK)
@@ -385,10 +387,7 @@ def tile_transformerblock_pa_kernel(
         rstd_of(1, sum_sq, rstd)
         for m in range(TOKEN_TILES):
             centre_and_scale(m)
-        keep_bias("scalar", b2_all, 2, b2_banks[2])
-        keep_bias("scalar", b2_all, 3, b2_banks[3])
-        fln_g_bank = spread("fln_g", 0, "odd")
-        fln_b_bank = spread("fln_b", 0, "odd")
+        regroup("scalar", 1, "B", 0, 320)
         row_sums = small.tile([P, TOKEN_TILES, 1], F32, tag="row_sums")
         minus_mean_2 = small.tile([P, TOKEN_TILES, 1], F32, tag="minus_mean")
         sum_sq_2 = small.tile([P, TOKEN_TILES, 1], F32, tag="sum_sq")
@@ -410,7 +409,8 @@ def tile_transformerblock_pa_kernel(
         rstd_of(0, sum_sq_2, rstd_2)
         square_sum(1, r[1], minus_mean_2, sum_sq_2)
         rstd_of(1, sum_sq_2, rstd_2)
-        regroup("scalar", 1, "B", 0, BANK)
+        regroup("scalar", 1, "B", 320, BANK)
+        regroup("scalar", 2, "B", 0, 224)
         centred = []
         for m in range(TOKEN_TILES):
             centred_row = rows.tile([P, D], F32, tag="row")
@@ -425,24 +425,20 @@ def tile_transformerblock_pa_kernel(
                 out=h2[:], in0=centred[m][:], scalar=rstd_2[:, m, :], in1=fln_b_bank[:], op0=ALU.mult, op1=ALU.add
             )
             h2_flipped.append(flip_tokens(h2[:]))
-        h2_grouped = [group_tokens(h2_flipped[0])]
-        regroup("scalar", 2, "B", 0, 224)
-        h2_grouped.append(group_tokens(h2_flipped[1]))
+        h2_grouped = [group_tokens(h2_flipped[m]) for m in range(TOKEN_TILES)]
         regroup("scalar", 2, "A", VECTOR_COLS[2], BANK)
-        regroup("vector", 1, "A", 0, 128)
-        regroup("vector", 2, "A", 0, VECTOR_COLS[2])
         quantise(1, "A")
+        regroup("vector", 3, "A", 0, VECTOR_COLS[3])
         h2_q = [quantise_tokens("h2_%d" % m, h2_grouped[m]) for m in range(TOKEN_TILES)]
         load_next()
         load_next()
+        nc.sync.dma_start(out=b2_all[:], in_=b2.partition_broadcast(P))
 
         for c in range(1, last + 2):
             if 3 < c + 1 <= last:
                 regroup("vector", c + 1, "A", 0, VECTOR_COLS[c + 1])
             if c <= last:
                 quantise_and_multiply(c, h2_q)
-            if c == 1:
-                regroup("vector", 3, "A", 0, VECTOR_COLS[3])
             if 2 < c + 1 <= last:
                 regroup("pool", c + 1, "B", CHUNK - POOL_COLS[c + 1] // 2, CHUNK)
             if c + 2 <= last:

@@ -26,10 +26,10 @@ RAW_BUFS = 6
 ROW_BUFS = 12
 RUN = 4
 EPS = 1e-5
-VECTOR_COLS = [0, 0, 0, 192, 192, 192, 192, 192, 192]
+VECTOR_COLS = [0, 0, 0, 160, 160, 160, 160, 160, 160]
 HEAD_A = 704
 HEAD_B = 704
-POOL_COLS = [0, 512, 512, 512, 512, 512, 512, 512, 512]
+POOL_COLS = [0, 512, 512, 640, 640, 640, 640, 640, 640]
 
 FLOPS = 2 * TOKENS * D * (D + 2 * F)
 

@@ -265,6 +265,7 @@ def tile_transformerblock_pa_kernel(
         rows_of_bo = consts.tile([P, BANK], BF16)
         rows_of_b1 = consts.tile([P, BANK], BF16)
         rows_of_norms = consts.tile([P, BANK], BF16)
+        rows_of_b2 = consts.tile([P, BANK], BF16)
         nc.gpsimd.memset(rows_of_bo[:].bitcast(U32), 0)
         eps_column = consts.tile([P, 1], F32)
         nc.gpsimd.memset(eps_column[:], EPS)
@@ -272,6 +273,7 @@ def tile_transformerblock_pa_kernel(
         make_identity(nc, ident[:])
         nc.vector.memset(rows_of_b1[:].bitcast(U32), 0)
         nc.vector.memset(rows_of_norms[:].bitcast(U32), 0)
+        nc.vector.memset(rows_of_b2[:].bitcast(U32), 0)
         ident_words = consts.tile([P, P], F32)
         make_identity(nc, ident_words[:])
 
@@ -296,6 +298,7 @@ def tile_transformerblock_pa_kernel(
             )
         )
         load_vectors(rows_of_norms, [("ln2_g", ln2_g), ("ln2_b", ln2_b), ("fln_g", fln_g), ("fln_b", fln_b)])
+        load_vectors(rows_of_b2, [("b2", b2)])
         warm = consts.tile([P, 1], F32)
         nc.scalar.activation(out=warm[:], in_=eps_column[:], func=ACT.Abs_reciprocal_sqrt)
         b1_all = consts.tile([P, F], BF16)
@@ -387,6 +390,7 @@ def tile_transformerblock_pa_kernel(
         rstd_of(1, sum_sq, rstd)
         for m in range(TOKEN_TILES):
             centre_and_scale(m)
+        b2_banks = [spread("b2", 0, "odd")]
         regroup("scalar", 1, "B", 0, 320)
         row_sums = small.tile([P, TOKEN_TILES, 1], F32, tag="row_sums")
         minus_mean_2 = small.tile([P, TOKEN_TILES, 1], F32, tag="minus_mean")
@@ -403,6 +407,7 @@ def tile_transformerblock_pa_kernel(
                 accum_out=row_sums[:, m, :],
             )
             nc.sync.dma_start(out=r_out[m, :, :], in_=r[m][:])
+        b2_banks.append(spread("b2", 1, "odd"))
         mean_of(0, row_sums[:, 0, :], 1, minus_mean_2)
         square_sum(0, r[0], minus_mean_2, sum_sq_2)
         mean_of(1, row_sums[:, 1, :], 1, minus_mean_2)
@@ -418,6 +423,8 @@ def tile_transformerblock_pa_kernel(
                 out=centred_row[:], in0=r[m][:], scalar=minus_mean_2[:, m, :], in1=fln_g_bank[:], op0=ALU.add, op1=ALU.mult
             )
             centred.append(centred_row)
+        b2_banks.append(spread("b2", 2, "odd"))
+        keep_bias("scalar", b2_all, 0, b2_banks[0])
         h2_flipped = []
         for m in range(TOKEN_TILES):
             h2 = acts.tile([P, D], BF16, tag="h2")
@@ -425,14 +432,18 @@ def tile_transformerblock_pa_kernel(
                 out=h2[:], in0=centred[m][:], scalar=rstd_2[:, m, :], in1=fln_b_bank[:], op0=ALU.mult, op1=ALU.add
             )
             h2_flipped.append(flip_tokens(h2[:]))
-        h2_grouped = [group_tokens(h2_flipped[m]) for m in range(TOKEN_TILES)]
+        b2_banks.append(spread("b2", 3, "odd"))
+        h2_grouped = [group_tokens(h2_flipped[0])]
+        keep_bias("scalar", b2_all, 1, b2_banks[1])
+        h2_grouped.append(group_tokens(h2_flipped[1]))
         regroup("scalar", 2, "A", VECTOR_COLS[2], BANK)
+        keep_bias("scalar", b2_all, 2, b2_banks[2])
+        keep_bias("scalar", b2_all, 3, b2_banks[3])
         quantise(1, "A")
         regroup("vector", 3, "A", 0, VECTOR_COLS[3])
         h2_q = [quantise_tokens("h2_%d" % m, h2_grouped[m]) for m in range(TOKEN_TILES)]
         load_next()
         load_next()
-        nc.sync.dma_start(out=b2_all[:], in_=b2.partition_broadcast(P))
 
         for c in range(1, last + 2):
             if 3 < c + 1 <= last:

from contextlib import ExitStack

import concourse.mybir as mybir
from concourse.masks import make_identity

F32 = mybir.dt.float32
BF16 = mybir.dt.bfloat16
U32 = mybir.dt.uint32
U8 = mybir.dt.uint8
FP8X4 = mybir.dt.float8_e4m3fn_x4
ALU = mybir.AluOpType
ACT = mybir.ActivationFunctionType

P = 128
PACK = 4
K_PASS = P * PACK
TOKENS = 256
TOKEN_TILES = TOKENS // P
D = 1024
F = 4096
PASSES = D // K_PASS
BANK = 512
CHUNK = 1024
SINGLE_CHUNKS = 3
RAW_BUFS = 6
ROW_BUFS = 12
RUN = 4
EPS = 1e-5
VECTOR_COLS = [0, 0, 0, 160, 160, 160, 160, 160, 160]
HEAD_A = 704
HEAD_B = 704
POOL_COLS = [0, 512, 512, 640, 640, 640, 640, 640, 640]

FLOPS = 2 * TOKENS * D * (D + 2 * F)


def tile_transformerblock_pa_kernel(
    tc, h_attn, x, Wo, bo, ln2_g, ln2_b, fln_g, fln_b, W1, b1, W2, b2, out_0, out_1, out_2
):
    nc = tc.nc
    r_out = out_0.flatten_outer_dims().rearrange("(p m) d -> m p d", p=P)

    chunks = [(Wo, 0)]
    for w in (W1, W2):
        for first_col in range(0, F, CHUNK):
            chunks.append((w, first_col))
    last = len(chunks) - 1
    units = [(c, None) for c in range(SINGLE_CHUNKS)]
    for c in range(SINGLE_CHUNKS, last + 1, 2):
        units += [(c, g) for g in range(PASSES)]
    pieces = {"A": (0, 0, CHUNK), "B": (1, 0, CHUNK)}

    with ExitStack() as ctx:
        consts = ctx.enter_context(tc.tile_pool(name="consts", bufs=1))
        small = ctx.enter_context(tc.tile_pool(name="small", bufs=2))
        rows = ctx.enter_context(tc.tile_pool(name="rows", bufs=ROW_BUFS))
        acts = ctx.enter_context(tc.tile_pool(name="acts", bufs=2))
        raw_pool = ctx.enter_context(tc.tile_pool(name="raw", bufs=RAW_BUFS))
        grouped_pool = ctx.enter_context(tc.tile_pool(name="grouped", bufs=2))
        quantised = ctx.enter_context(tc.tile_pool(name="quantised", bufs=2))
        psum = ctx.enter_context(tc.psum_pool(name="psum", bufs=4))
        ctx.enter_context(tc.manual_schedule())

        raw = {}
        grouped = {}
        packed = {}
        banks = {}
        loaded = []

        def load_next(between=None):
            if len(loaded) == len(units):
                return
            c, g = units[len(loaded)]
            w, first_col = chunks[c]
            if g is None:
                rows_of_chunk = raw_pool.tile([P, PASSES, PACK, CHUNK], BF16, tag="raw")
                for g in range(PASSES):
                    nc.sync.dma_start(
                        out=rows_of_chunk[:, g, :, :],
                        in_=w[g * K_PASS : (g + 1) * K_PASS, first_col : first_col + CHUNK].rearrange(
                            "(p t) n -> p t n", p=P
                        ),
                    )
                    raw[(c, g)] = rows_of_chunk[:, g, :, :]
                    if between and g == 0:
                        between()
            else:
                rows_of_pass = raw_pool.tile([P, PACK, 2 * CHUNK], BF16, tag="raw")
                nc.sync.dma_start(
                    out=rows_of_pass[:],
                    in_=w[g * K_PASS : (g + 1) * K_PASS, first_col : first_col + 2 * CHUNK].rearrange(
                        "(p t) n -> p t n", p=P
                    ),
                )
                for i in range(2):
                    raw[(c + i, g)] = rows_of_pass[:, :, i * CHUNK : (i + 1) * CHUNK]
            loaded.append(c)

        def spread(key, i, tag):
            vec_rows, first = first_row[key]
            bank = psum.tile([P, 2 * BANK], BF16, tag=tag)
            for s in range(2):
                row = first + 2 * i + s
                nc.tensor.matmul(
                    out=bank[:, s * BANK : (s + 1) * BANK],
                    lhsT=ident[:, row : row + 1].to_broadcast([P, P]),
                    rhs=vec_rows[:],
                    start=True,
                    stop=True,
                )
            return bank

        def keep_bias(engine, bias, i, bank):
            dst = bias[:, i * 2 * BANK : (i + 1) * 2 * BANK]
            if engine == "vector":
                nc.vector.tensor_copy(out=dst, in_=bank[:])
            else:
                nc.scalar.copy(out=dst, in_=bank[:])

        def flip_tokens(token_rows):
            words = token_rows.bitcast(F32)
            flipped = psum.tile([P, PASSES * 2, P], F32, tag="even")
            for g in range(PASSES):
                for u in range(2):
                    nc.tensor.transpose(
                        flipped[:, 2 * g + u, :],
                        words[:, g * 2 * P + u : (g + 1) * 2 * P : 2],
                        ident_words[:],
                    )
            return flipped

        def group_tokens(flipped):
            token_grouped = acts.tile([P, PASSES, P, PACK], BF16, tag="token_grouped", align_bytes=64)
            nc.scalar.copy(
                out=token_grouped[:].bitcast(F32),
                in_=flipped[:].rearrange("p (g u) r -> p g r u", u=2),
            )
            return token_grouped

        def quantise_tokens(key, token_grouped):
            codes = consts.tile([P, PASSES * P], U32, name="codes_" + key, align_bytes=64)
            scales = consts.tile([P, PASSES * P], U8, name="scales_" + key, align_bytes=64)
            nc.vector.quantize_mx(
                out=codes[:].bitcast(FP8X4),
                scales=scales[:],
                in_=token_grouped[:].rearrange("p g r t -> p (g r t)"),
            )
            return codes, scales

        def regroup(engine, c, piece, lo, hi):
            if lo >= hi:
                return
            g, first, width = pieces[piece]
            if (c, piece) not in grouped:
                slot = piece + str(c % 2)
                if c == 0:
                    slot = "B1" if piece == "A" else "A1"
                side_by_side = grouped_pool.tile([P, width, PACK], BF16, tag=slot, bufs=1, align_bytes=64)
                grouped[(c, piece)] = side_by_side
            dst = grouped[(c, piece)][:, lo:hi, :]
            src = raw[(c, g)][:, :, first + lo : first + hi]
            if engine == "pool":
                nc.gpsimd.tensor_scalar(
                    out=dst,
                    in0=src.rearrange("p t n -> p n t"),
                    scalar1=1.0,
                    scalar2=0.0,
                    op0=ALU.mult,
                    op1=ALU.add,
                )
                return
            dst = dst.rearrange("p (c i) t -> p c t i", i=RUN)
            src = src.rearrange("p t (c i) -> p c t i", i=RUN)
            if engine == "vector":
                nc.vector.tensor_copy(out=dst, in_=src)
            else:
                nc.scalar.copy(out=dst, in_=src)

        def quantise(c, piece):
            g, first, width = pieces[piece]
            if c not in packed:
                codes = quantised.tile([P, PASSES, CHUNK], U32, tag="codes", align_bytes=64)
                scales = quantised.tile([P, PASSES, CHUNK], U8, tag="scales", align_bytes=64)
                packed[c] = (codes, scales)
            codes, scales = packed[c]
            nc.vector.quantize_mx(
                out=codes[:, g, first : first + width].bitcast(FP8X4),
                scales=scales[:, g, first : first + width],
                in_=grouped[(c, piece)][:].rearrange("p n t -> p (n t)"),
            )

        def multiply(c, piece, m, tokens_q):
            g, first, width = pieces[piece]
            codes, scales = packed[c]
            token_codes, token_scales = tokens_q[m]
            for n in range(CHUNK // BANK):
                opened = (c, m, n) in banks
                if not opened:
                    acc = psum.tile([P, BANK], F32, tag=("odd" if c % 2 == 0 and c > 0 else "even"))
                    banks[(c, m, n)] = acc
                nc.tensor.matmul_mx(
                    out=banks[(c, m, n)][:],
                    lhsT=token_codes[:, g * P : (g + 1) * P].bitcast(FP8X4),
                    lhsT_scale=token_scales[:, g * P : (g + 1) * P],
                    rhs=codes[:, g, n * BANK : (n + 1) * BANK].bitcast(FP8X4),
                    rhs_scale=scales[:, g, n * BANK : (n + 1) * BANK],
                    start=not opened,
                    stop=opened,
                )

        def quantise_and_multiply(c, tokens_q):
            if c > 1:
                quantise(c, "A")
            multiply(c, "A", 0, tokens_q)
            if c == last:
                empty_bank(c - 1, 1, 0)
            quantise(c, "B")
            multiply(c, "B", 0, tokens_q)
            multiply(c, "A", 1, tokens_q)
            multiply(c, "B", 1, tokens_q)

        def square_sum(m, src, minus_mean, sum_sq):
            squares = acts.tile([P, D], BF16, tag="squares")
            nc.scalar.activation(
                out=squares[:],
                in_=src[:],
                func=ACT.Square,
                bias=minus_mean[:, m, :],
                accum_out=sum_sq[:, m, :],
            )

        def rstd_of(m, sum_sq, rstd):
            nc.scalar.activation(
                out=rstd[:, m, :],
                in_=sum_sq[:, m, :],
                func=ACT.Abs_reciprocal_sqrt,
                scale=1.0 / D,
                bias=eps_column[:],
            )

        staged = {}

        def empty_bank(c, m, n):
            w, first_col = chunks[c]
            out, bias = (out_1, b1_all) if w is W1 else (out_2, b2_all)
            if (c, m) not in staged:
                sums_and_bias = rows.tile([P, CHUNK], F32, tag="row")
                staged[(c, m)] = sums_and_bias
            nc.vector.tensor_tensor(
                out=staged[(c, m)][:, n * BANK : (n + 1) * BANK],
                in0=banks[(c, m, n)][:],
                in1=bias[:, first_col + n * BANK : first_col + (n + 1) * BANK],
                op=ALU.add,
            )
            out_rows = out.flatten_outer_dims().rearrange("(p m) f -> m p f", p=P)[m, :, :]
            if c == last:
                nc.sync.dma_start(
                    out=out_rows[:, first_col + n * BANK : first_col + (n + 1) * BANK],
                    in_=staged[(c, m)][:, n * BANK : (n + 1) * BANK],
                )
            elif n == CHUNK // BANK - 1:
                nc.sync.dma_start(out=out_rows[:, first_col : first_col + CHUNK], in_=staged[(c, m)][:])

        first_row = {}
        rows_of_bo = consts.tile([P, BANK], BF16)
        rows_of_b1 = consts.tile([P, BANK], BF16)
        rows_of_norms = consts.tile([P, BANK], BF16)
        rows_of_b2 = consts.tile([P, BANK], BF16)
        nc.gpsimd.memset(rows_of_bo[:].bitcast(U32), 0)
        eps_column = consts.tile([P, 1], F32)
        nc.gpsimd.memset(eps_column[:], EPS)
        ident = consts.tile([P, P], BF16)
        make_identity(nc, ident[:])
        nc.vector.memset(rows_of_b1[:].bitcast(U32), 0)
        nc.vector.memset(rows_of_norms[:].bitcast(U32), 0)
        nc.vector.memset(rows_of_b2[:].bitcast(U32), 0)
        ident_words = consts.tile([P, P], F32)
        make_identity(nc, ident_words[:])

        def load_vectors(vec_rows, vectors):
            row = 0
            for key, vec in vectors:
                n_rows = vec.shape[0] // BANK
                nc.sync.dma_start(out=vec_rows[row : row + n_rows, :], in_=vec.rearrange("(r c) -> r c", c=BANK))
                first_row[key] = (vec_rows, row)
                row += n_rows

        x_sb = rows.tile([P, D // BANK, TOKEN_TILES, BANK], BF16, tag="row")
        x_view = x.flatten_outer_dims().rearrange("(p m) d -> p m d", p=P)
        nc.sync.dma_start(out=x_sb[:, 0, :, :], in_=x_view[:, :, 0:BANK])
        load_vectors(rows_of_bo, [("bo", bo)])
        nc.sync.dma_start(out=x_sb[:, 1, :, :], in_=x_view[:, :, BANK:D])
        load_vectors(rows_of_b1, [("b1", b1)])
        h_sb = rows.tile([P, TOKEN_TILES, D], BF16, tag="row")
        load_next(
            between=lambda: nc.sync.dma_start(
                out=h_sb[:], in_=h_attn.flatten_outer_dims().rearrange("(p m) d -> p m d", p=P)
            )
        )
        load_vectors(rows_of_norms, [("ln2_g", ln2_g), ("ln2_b", ln2_b), ("fln_g", fln_g), ("fln_b", fln_b)])
        load_vectors(rows_of_b2, [("b2", b2)])
        warm = consts.tile([P, 1], F32)
        nc.scalar.activation(out=warm[:], in_=eps_column[:], func=ACT.Abs_reciprocal_sqrt)
        b1_all = consts.tile([P, F], BF16)
        b2_all = consts.tile([P, F], BF16)
        for i in range(RAW_BUFS - 1):
            load_next()

        bo_bank = spread("bo", 0, "even")
        x_plus_bo = [rows.tile([P, D], F32, tag="row", name="x_plus_bo%d" % m) for m in range(TOKEN_TILES)]
        for n in range(D // BANK):
            cols = slice(n * BANK, (n + 1) * BANK)
            for m in range(TOKEN_TILES):
                nc.vector.tensor_tensor(
                    out=x_plus_bo[m][:, cols], in0=x_sb[:, n, m, :], in1=bo_bank[:, cols], op=ALU.add
                )
        b1_banks = [spread("b1", i, "odd") for i in range(4)]
        keep_bias("scalar", b1_all, 0, b1_banks[0])
        regroup("scalar", 0, "A", HEAD_A, CHUNK)
        regroup("vector", 0, "A", 0, HEAD_A)
        h_flipped = [flip_tokens(h_sb[:, m, :]) for m in range(TOKEN_TILES)]
        h_grouped = [group_tokens(h_flipped[m]) for m in range(TOKEN_TILES)]
        quantise(0, "A")
        h_q = [quantise_tokens("h%d" % m, h_grouped[m]) for m in range(TOKEN_TILES)]
        multiply(0, "A", 0, h_q)
        multiply(0, "A", 1, h_q)
        ln2_g_bank = spread("ln2_g", 0, "odd")
        keep_bias("scalar", b1_all, 1, b1_banks[1])
        ln2_b_bank = spread("ln2_b", 0, "odd")
        regroup("scalar", 0, "B", HEAD_B, CHUNK)
        regroup("vector", 0, "B", 0, HEAD_B)
        quantise(0, "B")
        multiply(0, "B", 0, h_q)
        multiply(0, "B", 1, h_q)
        keep_bias("scalar", b1_all, 2, b1_banks[2])
        keep_bias("scalar", b1_all, 3, b1_banks[3])
        fln_g_bank = spread("fln_g", 0, "odd")
        fln_b_bank = spread("fln_b", 0, "odd")
        regroup("scalar", 1, "A", 0, BANK)
        load_next()

        regroup("pool", 1, "A", BANK, CHUNK)
        regroup("pool", 1, "B", BANK, CHUNK)
        regroup("pool", 2, "A", BANK, CHUNK)
        regroup("pool", 2, "B", CHUNK - POOL_COLS[2], CHUNK)
        regroup("pool", 2, "B", 224, CHUNK - POOL_COLS[2])
        half_sums = small.tile([P, TOKEN_TILES, 2], F32, tag="half_sums")
        scaled_halves = small.tile([P, TOKEN_TILES, 2], F32, tag="scaled_halves")
        minus_mean = small.tile([P, TOKEN_TILES, 1], F32, tag="minus_mean")
        sum_sq = small.tile([P, TOKEN_TILES, 1], F32, tag="sum_sq")
        rstd = small.tile([P, TOKEN_TILES, 1], F32, tag="rstd")
        y = [rows.tile([P, D], F32, tag="row", name="y%d" % m) for m in range(TOKEN_TILES)]
        r = y
        scaled = x_plus_bo

        def add_residual(m, n):
            cols = slice(n * BANK, (n + 1) * BANK)
            nc.vector.scalar_tensor_tensor(
                out=y[m][:, cols],
                in0=banks[(0, m, n)][:],
                scalar=1.0,
                in1=x_plus_bo[m][:, cols],
                op0=ALU.mult,
                op1=ALU.add,
                accum_out=half_sums[:, m, n : n + 1],
            )

        def centre_and_scale(m):
            nc.vector.scalar_tensor_tensor(
                out=scaled[m][:], in0=y[m][:], scalar=minus_mean[:, m, :], in1=ln2_g_bank[:], op0=ALU.add, op1=ALU.mult
            )

        def mean_of(m, sums, parts, minus_mean):
            nc.scalar.activation(
                out=scaled_halves[:, m, 0:parts],
                in_=sums,
                func=ACT.Copy,
                scale=-1.0 / D,
                accum_out=minus_mean[:, m, :],
            )

        for m in range(TOKEN_TILES):
            for n in range(D // BANK):
                add_residual(m, n)
        mean_of(0, half_sums[:, 0, :], 2, minus_mean)
        square_sum(0, y[0], minus_mean, sum_sq)
        mean_of(1, half_sums[:, 1, :], 2, minus_mean)
        rstd_of(0, sum_sq, rstd)
        square_sum(1, y[1], minus_mean, sum_sq)
        rstd_of(1, sum_sq, rstd)
        for m in range(TOKEN_TILES):
            centre_and_scale(m)
        b2_banks = [spread("b2", 0, "odd")]
        regroup("scalar", 1, "B", 0, 320)
        row_sums = small.tile([P, TOKEN_TILES, 1], F32, tag="row_sums")
        minus_mean_2 = small.tile([P, TOKEN_TILES, 1], F32, tag="minus_mean")
        sum_sq_2 = small.tile([P, TOKEN_TILES, 1], F32, tag="sum_sq")
        rstd_2 = small.tile([P, TOKEN_TILES, 1], F32, tag="rstd")
        for m in range(TOKEN_TILES):
            nc.vector.scalar_tensor_tensor(
                out=r[m][:],
                in0=scaled[m][:],
                scalar=rstd[:, m, :],
                in1=ln2_b_bank[:],
                op0=ALU.mult,
                op1=ALU.add,
                accum_out=row_sums[:, m, :],
            )
            nc.sync.dma_start(out=r_out[m, :, :], in_=r[m][:])
        b2_banks.append(spread("b2", 1, "odd"))
        mean_of(0, row_sums[:, 0, :], 1, minus_mean_2)
        square_sum(0, r[0], minus_mean_2, sum_sq_2)
        mean_of(1, row_sums[:, 1, :], 1, minus_mean_2)
        rstd_of(0, sum_sq_2, rstd_2)
        square_sum(1, r[1], minus_mean_2, sum_sq_2)
        rstd_of(1, sum_sq_2, rstd_2)
        regroup("scalar", 1, "B", 320, BANK)
        regroup("scalar", 2, "B", 0, 224)
        centred = []
        for m in range(TOKEN_TILES):
            centred_row = rows.tile([P, D], F32, tag="row")
            nc.vector.scalar_tensor_tensor(
                out=centred_row[:], in0=r[m][:], scalar=minus_mean_2[:, m, :], in1=fln_g_bank[:], op0=ALU.add, op1=ALU.mult
            )
            centred.append(centred_row)
        b2_banks.append(spread("b2", 2, "odd"))
        keep_bias("scalar", b2_all, 0, b2_banks[0])
        h2_flipped = []
        for m in range(TOKEN_TILES):
            h2 = acts.tile([P, D], BF16, tag="h2")
            nc.vector.scalar_tensor_tensor(
                out=h2[:], in0=centred[m][:], scalar=rstd_2[:, m, :], in1=fln_b_bank[:], op0=ALU.mult, op1=ALU.add
            )
            h2_flipped.append(flip_tokens(h2[:]))
        b2_banks.append(spread("b2", 3, "odd"))
        h2_grouped = [group_tokens(h2_flipped[0])]
        keep_bias("scalar", b2_all, 1, b2_banks[1])
        h2_grouped.append(group_tokens(h2_flipped[1]))
        regroup("scalar", 2, "A", VECTOR_COLS[2], BANK)
        keep_bias("scalar", b2_all, 2, b2_banks[2])
        keep_bias("scalar", b2_all, 3, b2_banks[3])
        quantise(1, "A")
        regroup("vector", 3, "A", 0, VECTOR_COLS[3])
        h2_q = [quantise_tokens("h2_%d" % m, h2_grouped[m]) for m in range(TOKEN_TILES)]
        load_next()
        load_next()

        for c in range(1, last + 2):
            if 3 < c + 1 <= last:
                regroup("vector", c + 1, "A", 0, VECTOR_COLS[c + 1])
            if c <= last:
                quantise_and_multiply(c, h2_q)
            if 2 < c + 1 <= last:
                regroup("pool", c + 1, "B", CHUNK - POOL_COLS[c + 1] // 2, CHUNK)
            if c + 2 <= last:
                regroup("pool", c + 2, "B", CHUNK - POOL_COLS[c + 2], CHUNK - POOL_COLS[c + 2] // 2)
            if c + 1 <= last:
                regroup("scalar", c + 1, "A", CHUNK if c + 1 == 2 else VECTOR_COLS[c + 1], CHUNK)
                if c + 1 > 2:
                    regroup("scalar", c + 1, "B", 0, CHUNK - POOL_COLS[c + 1])
            for cc, m in ((c - 1, 1), (c, 0)):
                if 1 <= cc <= last:
                    for n in range(CHUNK // BANK):
                        if (cc, m, n) != (last - 1, 1, 0):
                            empty_bank(cc, m, n)
